import numpy as np
import ml_dtypes


def mxq(x, axis, fmt="e4m3"):
    dtype, down = {"e4m3": (ml_dtypes.float8_e4m3fn, 7), "e5m2": (ml_dtypes.float8_e5m2, 14)}[fmt]
    v = np.moveaxis(np.asarray(x, np.float32).astype(ml_dtypes.bfloat16).astype(np.float64), axis, -1)
    blocks = v.reshape(v.shape[:-1] + (-1, 32))
    amax = np.abs(blocks).max(-1, keepdims=True)
    byte = np.maximum(np.where(amax > 0, np.frexp(amax)[1] - 1 + 127, 0) - down, 1)
    scale = np.exp2(byte - 127.0)
    codes = (blocks / scale).astype(np.float32).astype(dtype).astype(np.float64)
    return np.moveaxis((codes * scale).reshape(v.shape), -1, axis)


WIDE = False


def mx_kscale(k):
    if not WIDE:
        return np.ones(k)
    levels = np.array([10, -10, 5, -5, 0])
    a = np.random.permutation(np.resize(levels, k // 512 * 4)).reshape(k // 512, 4)
    idx = np.arange(k)
    return np.exp2(a[idx // 512, idx % 128 // 32])


BF16 = ml_dtypes.bfloat16


def bf(x):
    return np.asarray(x, np.float32).astype(BF16)


def f64(x):
    return np.asarray(x).astype(np.float64)


B, T, H, HD, W, G = 1, 1536, 8, 128, 512, 512
D = H * HD
NW = T // W


def setup_inputs():
    s = mx_kscale(D)
    return {"x": bf(np.random.standard_normal((B, T, D)) * s),
            "Wv": bf(np.random.standard_normal((D, D)) * 2.0 / np.sqrt(D) / s[None, :]),
            "q": bf(np.random.standard_normal((B, H, T, HD)) * 1.4),
            "k": bf(np.random.standard_normal((B, H, T, HD)) * 1.4)}


def reference(x, Wv, q, k):
    scale = HD ** -0.5
    v = (mxq(f64(x), 2, "e4m3") @ mxq(f64(Wv), 1, "e4m3").T).reshape(B, T, H, HD).transpose(0, 2, 1, 3)
    qw = f64(q).reshape(B, H, NW, W, HD)
    kk = f64(k)
    kw = kk.reshape(B, H, NW, W, HD)
    kg = kk[:, :, :G, :]
    s_g = (qw @ kg[:, :, None].transpose(0, 1, 2, 4, 3)) * scale
    s_l = (qw @ kw.transpose(0, 1, 2, 4, 3)) * scale
    s = np.concatenate([s_g, s_l], axis=-1)
    e = np.exp(s - s.max(-1, keepdims=True))
    vq = mxq(v, 2, "e4m3")
    o = (mxq(e[..., :G], 4, "e4m3") @ vq[:, :, None, :G, :]) + (mxq(e[..., G:], 4, "e4m3") @ vq.reshape(B, H, NW, W, HD))
    o = o / e.sum(-1, keepdims=True)
    return o.reshape(B, H, T, HD).transpose(0, 2, 1, 3).reshape(B, T, D)

@@ -1,0 +1,371 @@
+from contextlib import ExitStack
+
+import concourse.mybir as mybir
+from concourse.masks import make_identity
+
+BF16 = mybir.dt.bfloat16
+F32 = mybir.dt.float32
+U32 = mybir.dt.uint32
+U8 = mybir.dt.uint8
+FP8X4 = mybir.dt.float8_e4m3fn_x4
+EXP = mybir.ActivationFunctionType.Exp
+ALU = mybir.AluOpType
+AXIS_X = mybir.AxisListType.X
+
+P = 128
+PACK = 4
+K_PASS = P * PACK
+HEADS = 8
+HEAD_DIM = 128
+SEQ = 1536
+FEATURES = 1024
+WINDOW = 512
+WINDOWS = SEQ // WINDOW
+ROW_TILES = SEQ // P
+TILES_PER_WINDOW = WINDOW // P
+FEATURE_PASSES = FEATURES // K_PASS
+WORD_SLABS = FEATURES // (2 * P)
+HEADS_PER_BANK = 4
+SCALE = HEAD_DIM**-0.5
+
+FLOPS = 2 * SEQ * FEATURES * FEATURES + 2 * (2 * HEADS * SEQ * 2 * WINDOW * HEAD_DIM)
+
+
+def tile_hybridattention_pa_kernel(tc, x, Wv, q, k, out):
+    nc = tc.nc
+    x_rows = x.flatten_outer_dims()
+    out_rows = out.flatten_outer_dims()
+    q_heads = q.rearrange("b h t d -> (b h) t d")
+    k_heads = k.rearrange("b h t d -> (b h) t d")
+
+    with ExitStack() as stack:
+        stack.enter_context(tc.manual_schedule())
+        keep = stack.enter_context(tc.tile_pool(name="keep", bufs=1))
+        stage = stack.enter_context(tc.tile_pool(name="stage", bufs=3))
+        small = stack.enter_context(tc.tile_pool(name="small", bufs=4))
+        psum_plain = stack.enter_context(tc.psum_pool(name="psum_plain", bufs=4))
+        psum_flip = stack.enter_context(tc.psum_pool(name="psum_flip", bufs=2))
+        psum_mx = stack.enter_context(tc.psum_pool(name="psum_mx", bufs=2))
+
+        w_raw = keep.tile([P, HEADS, FEATURES], BF16)
+        w_view = Wv.rearrange("(h p) i -> p h i", p=P)
+        for h in range(0, HEADS, 2):
+            nc.sync.dma_start(out=w_raw[:, h : h + 2, :], in_=w_view[:, h : h + 2, :])
+        x_raw = keep.tile([P, ROW_TILES // 2, 2, FEATURES], BF16)
+        for c in range(ROW_TILES // 2):
+            nc.sync.dma_start(
+                out=x_raw[:, c],
+                in_=x_rows[2 * P * c : 2 * P * (c + 1), :].rearrange("(p e) i -> p e i", e=2),
+            )
+        k_raw = keep.tile([P, HEADS, ROW_TILES, HEAD_DIM], BF16)
+        for h in range(0, HEADS, 2):
+            nc.sync.dma_start(
+                out=k_raw[:, h : h + 2].rearrange("p h a d -> p (h a) d"),
+                in_=k_heads[h : h + 2].rearrange("h (a p) d -> p (h a) d", p=P),
+            )
+        q_raw = keep.tile([P, HEADS, WINDOWS, TILES_PER_WINDOW, HEAD_DIM], BF16)
+        for h in range(0, HEADS, 2):
+            nc.sync.dma_start(
+                out=q_raw[:, h : h + 2].rearrange("p h w r d -> p (h w) (r d)"),
+                in_=q_heads[h : h + 2].rearrange(
+                    "h (w p r) d -> p (h w) (r d)", w=WINDOWS, p=P, r=TILES_PER_WINDOW
+                ),
+            )
+
+        ident_f32 = keep.tile([P, P], F32)
+        make_identity(nc, ident_f32[:])
+        ident_bf16 = keep.tile([P, P], BF16)
+        make_identity(nc, ident_bf16[:])
+
+        zero = keep.tile([P, 1], F32)
+        nc.vector.memset(zero[:], 0.0)
+        one = keep.tile([P, 1], F32)
+        nc.scalar.activation(out=one[:], in_=zero[:], func=EXP)
+
+        def pipeline(jobs, stages):
+            for step in range(jobs + len(stages) - 1):
+                for lag, stage_fn in enumerate(stages):
+                    if 0 <= step - lag < jobs:
+                        stage_fn(step - lag)
+
+        w_codes = keep.tile([P, HEADS, FEATURE_PASSES, P], U32, align_bytes=64)
+        w_scales = keep.tile([P, HEADS, FEATURE_PASSES, P], U8, align_bytes=64)
+        x_codes = keep.tile([P, ROW_TILES, FEATURE_PASSES, P], U32, align_bytes=64)
+        x_scales = keep.tile([P, ROW_TILES, FEATURE_PASSES, P], U8, align_bytes=64)
+        feature_rows = [(w_raw[:, h, :], w_codes[:, h], w_scales[:, h]) for h in range(HEADS)]
+        feature_rows += [
+            (x_raw[:, n // 2, n % 2, :], x_codes[:, n], x_scales[:, n]) for n in range(ROW_TILES)
+        ]
+        flipped_rows = {}
+        grouped_rows = {}
+
+        def flip_rows(job):
+            words = feature_rows[job][0].bitcast(F32)
+            flipped = psum_plain.tile([P, WORD_SLABS, P], F32, tag="plain")
+            for slab in range(WORD_SLABS):
+                nc.tensor.transpose(
+                    flipped[:, slab, :], words[:, slab * P : (slab + 1) * P], ident_f32[:]
+                )
+            flipped_rows[job] = flipped
+
+        def group_rows(job):
+            grouped = stage.tile([P, FEATURE_PASSES, P, 2], F32, tag="grouped_rows", align_bytes=64)
+            nc.scalar.copy(
+                out=grouped[:],
+                in_=flipped_rows[job][:].rearrange("p (c u) t -> p c t u", u=2),
+            )
+            grouped_rows[job] = grouped
+
+        def quantise_rows(job):
+            nc.vector.quantize_mx(
+                out=feature_rows[job][1].rearrange("p c t -> p (c t)").bitcast(FP8X4),
+                scales=feature_rows[job][2].rearrange("p c t -> p (c t)"),
+                in_=grouped_rows[job][:].rearrange("p c t u -> p (c t u)").bitcast(BF16),
+            )
+
+        pipeline(len(feature_rows), [flip_rows, group_rows, quantise_rows])
+
+        v_codes = keep.tile([P, WINDOWS, HEADS, HEAD_DIM], U32, align_bytes=64)
+        v_scales = keep.tile([P, WINDOWS, HEADS, HEAD_DIM], U8, align_bytes=64)
+        v_sums = {}
+        v_grouped = {}
+
+        def project(job):
+            w, h = divmod(job, HEADS)
+            sums = psum_mx.tile([P, PACK, HEAD_DIM], F32, tag="mx")
+            for j in range(PACK):
+                for c in range(FEATURE_PASSES):
+                    nc.tensor.matmul_mx(
+                        out=sums[:, j, :],
+                        lhsT=x_codes[:, PACK * w + j, c, :].bitcast(FP8X4),
+                        lhsT_scale=x_scales[:, PACK * w + j, c, :],
+                        rhs=w_codes[:, h, c, :].bitcast(FP8X4),
+                        rhs_scale=w_scales[:, h, c, :],
+                        start=(c == 0),
+                        stop=(c == FEATURE_PASSES - 1),
+                    )
+            v_sums[job] = sums
+
+        def group_v(job):
+            grouped = stage.tile([P, HEAD_DIM, PACK], BF16, tag="v_grouped", align_bytes=64)
+            nc.scalar.copy(out=grouped[:], in_=v_sums[job][:].rearrange("p j d -> p d j"))
+            v_grouped[job] = grouped
+
+        def quantise_v(job):
+            w, h = divmod(job, HEADS)
+            nc.vector.quantize_mx(
+                out=v_codes[:, w, h, :].bitcast(FP8X4),
+                scales=v_scales[:, w, h, :],
+                in_=v_grouped[job][:].rearrange("p d j -> p (d j)"),
+            )
+
+        pipeline(WINDOWS * HEADS, [project, group_v, quantise_v])
+
+        kT = keep.tile([P, HEADS, SEQ], BF16)
+        qT = keep.tile([P, HEADS, WINDOWS, TILES_PER_WINDOW, P], BF16)
+        head_rows = [
+            (k_raw[:, h, TILES_PER_WINDOW * w : TILES_PER_WINDOW * (w + 1), :],
+             kT[:, h, WINDOW * w : WINDOW * (w + 1)])
+            for h in range(HEADS)
+            for w in range(WINDOWS)
+        ]
+        head_rows += [
+            (q_raw[:, h, w], qT[:, h, w].rearrange("d r p -> d (r p)"))
+            for h in range(HEADS)
+            for w in range(WINDOWS)
+        ]
+        flipped_heads = {}
+
+        def flip_heads(job):
+            flipped = psum_plain.tile([P, TILES_PER_WINDOW, P], BF16, tag="plain")
+            for a in range(TILES_PER_WINDOW):
+                nc.tensor.transpose(flipped[:, a, :], head_rows[job][0][:, a, :], ident_bf16[:])
+            flipped_heads[job] = flipped
+
+        def keep_heads(job):
+            nc.vector.tensor_copy(
+                out=head_rows[job][1], in_=flipped_heads[job][:].rearrange("d a p -> d (a p)")
+            )
+
+        pipeline(len(head_rows), [flip_heads, keep_heads])
+
+        units = [
+            (w, r, h)
+            for w in range(WINDOWS)
+            for r in range(TILES_PER_WINDOW)
+            for h in range(HEADS)
+        ]
+
+        def key_windows(unit):
+            w = units[unit][0]
+            return [0] if w == 0 else [0, w]
+
+        score_banks = {}
+        maxima_of = {}
+        bias_of = {}
+        row_sums = {}
+        e_of = {}
+        flipped_e = {}
+        grouped_e = {}
+        e_codes = {}
+        e_scales = {}
+        products = {}
+        totals = {}
+        inverses = {}
+        results = {}
+
+        def scores(unit):
+            w, r, h = units[unit]
+            score_banks[unit] = []
+            for kw in key_windows(unit):
+                bank = psum_plain.tile([P, WINDOW], F32, tag="plain")
+                nc.tensor.matmul(
+                    out=bank[:],
+                    lhsT=qT[:, h, w, r, :],
+                    rhs=kT[:, h, WINDOW * kw : WINDOW * (kw + 1)],
+                    start=True,
+                    stop=True,
+                )
+                score_banks[unit].append(bank)
+
+        def row_maxima(unit):
+            maxima = small.tile([P, 2], F32, tag="maxima")
+            for g, bank in enumerate(score_banks[unit]):
+                nc.vector.tensor_reduce(out=maxima[:, g : g + 1], in_=bank[:], axis=AXIS_X, op=ALU.max)
+            maxima_of[unit] = maxima
+
+        def exp_bias(unit):
+            maxima = maxima_of[unit]
+            last = len(score_banks[unit]) - 1
+            bias = small.tile([P, 1], F32, tag="bias")
+            nc.vector.tensor_scalar(
+                out=bias[:],
+                in0=maxima[:, 0:1],
+                scalar1=maxima[:, last : last + 1],
+                scalar2=-SCALE,
+                op0=ALU.max,
+                op1=ALU.mult,
+            )
+            bias_of[unit] = bias
+
+        def exponentials(unit):
+            group, slot = divmod(unit, HEADS_PER_BANK)
+            if slot == 0:
+                sums = small.tile([P, HEADS_PER_BANK, 2], F32, tag="row_sums")
+                row_sums[group] = sums
+            bias = bias_of[unit]
+            e = stage.tile([P, 2 * WINDOW], BF16, tag="e")
+            for g, bank in enumerate(score_banks[unit]):
+                nc.scalar.activation(
+                    out=e[:, WINDOW * g : WINDOW * (g + 1)],
+                    in_=bank[:],
+                    func=EXP,
+                    bias=bias[:],
+                    scale=SCALE,
+                    accum_out=row_sums[group][:, slot, g : g + 1],
+                )
+            e_of[unit] = e
+
+        def flip_e(unit):
+            words = e_of[unit][:].bitcast(F32)
+            flipped = psum_flip.tile([P, 2, 2, P], F32, tag="flip")
+            for g in range(len(key_windows(unit))):
+                for u in range(2):
+                    slab = 2 * g + u
+                    nc.tensor.transpose(
+                        flipped[:, g, u, :], words[:, slab * P : (slab + 1) * P], ident_f32[:]
+                    )
+            flipped_e[unit] = flipped
+
+        def group_e(unit):
+            groups = len(key_windows(unit))
+            grouped = stage.tile([P, 2, P, 2], F32, tag="grouped_e", align_bytes=64)
+            nc.scalar.copy(
+                out=grouped[:, 0:groups],
+                in_=flipped_e[unit][:, 0:groups].rearrange("p g u q -> p g q u"),
+            )
+            grouped_e[unit] = grouped
+
+        def quantise_e(unit):
+            groups = len(key_windows(unit))
+            codes = stage.tile([P, 2 * P], U32, tag="e_codes", align_bytes=64)
+            scales = stage.tile([P, 2 * P], U8, tag="e_scales", align_bytes=64)
+            nc.vector.quantize_mx(
+                out=codes[:, 0 : groups * P].bitcast(FP8X4),
+                scales=scales[:, 0 : groups * P],
+                in_=grouped_e[unit][:, 0:groups].rearrange("p g q u -> p (g q u)").bitcast(BF16),
+            )
+            e_codes[unit] = codes
+            e_scales[unit] = scales
+
+        def multiply(unit):
+            h = units[unit][2]
+            group, slot = divmod(unit, HEADS_PER_BANK)
+            if slot == 0:
+                sums = psum_mx.tile([P, HEADS_PER_BANK, HEAD_DIM], F32, tag="mx")
+                products[group] = sums
+            codes = e_codes[unit]
+            scales = e_scales[unit]
+            windows = key_windows(unit)
+            for g, kw in enumerate(windows):
+                nc.tensor.matmul_mx(
+                    out=products[group][:, slot, :],
+                    lhsT=codes[:, g * P : (g + 1) * P].bitcast(FP8X4),
+                    lhsT_scale=scales[:, g * P : (g + 1) * P],
+                    rhs=v_codes[:, kw, h, :].bitcast(FP8X4),
+                    rhs_scale=v_scales[:, kw, h, :],
+                    start=(g == 0),
+                    stop=(g == len(windows) - 1),
+                )
+
+        def add_row_sums(group):
+            groups = len(key_windows(group * HEADS_PER_BANK))
+            total = small.tile([P, HEADS_PER_BANK], F32, tag="total")
+            nc.vector.tensor_reduce(
+                out=total[:], in_=row_sums[group][:, :, 0:groups], axis=AXIS_X, op=ALU.add
+            )
+            totals[group] = total
+
+        def invert_row_sums(group):
+            inverse = small.tile([P, HEADS_PER_BANK], F32, tag="inverse")
+            nc.vector.reciprocal(out=inverse[:], in_=totals[group][:])
+            inverses[group] = inverse
+
+        def normalise(group):
+            w, r, h = units[group * HEADS_PER_BANK]
+            if h == 0:
+                result = stage.tile([P, HEADS, HEAD_DIM], F32, tag="result")
+                results[(w, r)] = result
+            nc.vector.tensor_tensor(
+                out=results[(w, r)][:, h : h + HEADS_PER_BANK, :],
+                in0=products[group][:],
+                in1=inverses[group][:].unsqueeze(2).to_broadcast([P, HEADS_PER_BANK, HEAD_DIM]),
+                op=ALU.mult,
+            )
+            if h + HEADS_PER_BANK == HEADS:
+                window_rows = out_rows[WINDOW * w : WINDOW * (w + 1), :]
+                nc.sync.dma_start(
+                    out=window_rows.rearrange("(p r) n -> p r n", r=TILES_PER_WINDOW)[:, r, :],
+                    in_=results[(w, r)][:].rearrange("p h d -> p (h d)"),
+                )
+
+        def for_unit(stage_fn, unit):
+            if 0 <= unit < len(units):
+                stage_fn(unit)
+
+        def for_group(stage_fn, unit):
+            if 0 <= unit < len(units) and unit % HEADS_PER_BANK == HEADS_PER_BANK - 1:
+                stage_fn(unit // HEADS_PER_BANK)
+
+        for step in range(len(units) + 7):
+            for_unit(exponentials, step - 2)
+            for_unit(scores, step)
+            for_unit(flip_e, step - 2)
+            for_unit(group_e, step - 3)
+            for_unit(row_maxima, step - 1)
+            for_group(add_row_sums, step - 3)
+            for_unit(quantise_e, step - 4)
+            for_unit(exp_bias, step - 1)
+            for_group(invert_row_sums, step - 4)
+            for_unit(multiply, step - 5)
+            for_group(normalise, step - 6)

@@ -25,7 +25,7 @@ ROW_TILES = SEQ // P
 TILES_PER_WINDOW = WINDOW // P
 FEATURE_PASSES = FEATURES // K_PASS
 WORD_SLABS = FEATURES // (2 * P)
-HEADS_PER_BANK = 4
+WINDOW_ORDER = (1, 2, 0)
 SCALE = HEAD_DIM**-0.5
 
 FLOPS = 2 * SEQ * FEATURES * FEATURES + 2 * (2 * HEADS * SEQ * 2 * WINDOW * HEAD_DIM)
@@ -43,34 +43,32 @@ def tile_hybridattention_pa_kernel(tc, x, Wv, q, k, out):
         keep = stack.enter_context(tc.tile_pool(name="keep", bufs=1))
         stage = stack.enter_context(tc.tile_pool(name="stage", bufs=3))
         small = stack.enter_context(tc.tile_pool(name="small", bufs=4))
-        psum_plain = stack.enter_context(tc.psum_pool(name="psum_plain", bufs=4))
-        psum_flip = stack.enter_context(tc.psum_pool(name="psum_flip", bufs=2))
-        psum_mx = stack.enter_context(tc.psum_pool(name="psum_mx", bufs=2))
+        psum_scores = stack.enter_context(tc.psum_pool(name="psum_scores", bufs=4))
+        psum_work = stack.enter_context(tc.psum_pool(name="psum_work", bufs=4))
 
         w_raw = keep.tile([P, HEADS, FEATURES], BF16)
-        w_view = Wv.rearrange("(h p) i -> p h i", p=P)
-        for h in range(0, HEADS, 2):
-            nc.sync.dma_start(out=w_raw[:, h : h + 2, :], in_=w_view[:, h : h + 2, :])
-        x_raw = keep.tile([P, ROW_TILES // 2, 2, FEATURES], BF16)
-        for c in range(ROW_TILES // 2):
-            nc.sync.dma_start(
-                out=x_raw[:, c],
-                in_=x_rows[2 * P * c : 2 * P * (c + 1), :].rearrange("(p e) i -> p e i", e=2),
-            )
         k_raw = keep.tile([P, HEADS, ROW_TILES, HEAD_DIM], BF16)
-        for h in range(0, HEADS, 2):
-            nc.sync.dma_start(
-                out=k_raw[:, h : h + 2].rearrange("p h a d -> p (h a) d"),
-                in_=k_heads[h : h + 2].rearrange("h (a p) d -> p (h a) d", p=P),
-            )
         q_raw = keep.tile([P, HEADS, WINDOWS, TILES_PER_WINDOW, HEAD_DIM], BF16)
-        for h in range(0, HEADS, 2):
+        x_raw = keep.tile([P, ROW_TILES // 2, 2, FEATURES], BF16)
+        for h in range(HEADS):
+            nc.sync.dma_start(out=w_raw[:, h, :], in_=Wv[P * h : P * (h + 1), :])
             nc.sync.dma_start(
-                out=q_raw[:, h : h + 2].rearrange("p h w r d -> p (h w) (r d)"),
-                in_=q_heads[h : h + 2].rearrange(
-                    "h (w p r) d -> p (h w) (r d)", w=WINDOWS, p=P, r=TILES_PER_WINDOW
+                out=k_raw[:, h], in_=k_heads[h].rearrange("(a p) d -> p a d", p=P)
+            )
+            nc.sync.dma_start(
+                out=q_raw[:, h].rearrange("p w r d -> p w (r d)"),
+                in_=q_heads[h].rearrange(
+                    "(w p r) d -> p w (r d)", w=WINDOWS, p=P, r=TILES_PER_WINDOW
                 ),
             )
+            if h == 0:
+                for c in range(ROW_TILES // 2):
+                    nc.sync.dma_start(
+                        out=x_raw[:, c],
+                        in_=x_rows[2 * P * c : 2 * P * (c + 1), :].rearrange(
+                            "(p e) i -> p e i", e=2
+                        ),
+                    )
 
         ident_f32 = keep.tile([P, P], F32)
         make_identity(nc, ident_f32[:])
@@ -82,48 +80,44 @@ def tile_hybridattention_pa_kernel(tc, x, Wv, q, k, out):
         one = keep.tile([P, 1], F32)
         nc.scalar.activation(out=one[:], in_=zero[:], func=EXP)
 
-        def pipeline(jobs, stages):
-            for step in range(jobs + len(stages) - 1):
-                for lag, stage_fn in enumerate(stages):
-                    if 0 <= step - lag < jobs:
-                        stage_fn(step - lag)
-
         w_codes = keep.tile([P, HEADS, FEATURE_PASSES, P], U32, align_bytes=64)
         w_scales = keep.tile([P, HEADS, FEATURE_PASSES, P], U8, align_bytes=64)
         x_codes = keep.tile([P, ROW_TILES, FEATURE_PASSES, P], U32, align_bytes=64)
         x_scales = keep.tile([P, ROW_TILES, FEATURE_PASSES, P], U8, align_bytes=64)
-        feature_rows = [(w_raw[:, h, :], w_codes[:, h], w_scales[:, h]) for h in range(HEADS)]
-        feature_rows += [
-            (x_raw[:, n // 2, n % 2, :], x_codes[:, n], x_scales[:, n]) for n in range(ROW_TILES)
+        w_jobs = [
+            ("w", h, w_raw[:, h, :], w_codes[:, h], w_scales[:, h], nc.vector.tensor_copy)
+            for h in range(HEADS)
+        ]
+        x_jobs = [
+            ("x", n, x_raw[:, n // 2, n % 2, :], x_codes[:, n], x_scales[:, n], nc.scalar.copy)
+            for n in range(ROW_TILES)
         ]
         flipped_rows = {}
         grouped_rows = {}
 
         def flip_rows(job):
-            words = feature_rows[job][0].bitcast(F32)
-            flipped = psum_plain.tile([P, WORD_SLABS, P], F32, tag="plain")
+            words = job[2].bitcast(F32)
+            flipped = psum_work.tile([P, WORD_SLABS, P], F32, tag="work")
             for slab in range(WORD_SLABS):
                 nc.tensor.transpose(
                     flipped[:, slab, :], words[:, slab * P : (slab + 1) * P], ident_f32[:]
                 )
-            flipped_rows[job] = flipped
+            flipped_rows[job[0:2]] = flipped
 
         def group_rows(job):
             grouped = stage.tile([P, FEATURE_PASSES, P, 2], F32, tag="grouped_rows", align_bytes=64)
-            nc.scalar.copy(
+            job[5](
                 out=grouped[:],
-                in_=flipped_rows[job][:].rearrange("p (c u) t -> p c t u", u=2),
+                in_=flipped_rows[job[0:2]][:].rearrange("p (c u) t -> p c t u", u=2),
             )
-            grouped_rows[job] = grouped
+            grouped_rows[job[0:2]] = grouped
 
         def quantise_rows(job):
             nc.vector.quantize_mx(
-                out=feature_rows[job][1].rearrange("p c t -> p (c t)").bitcast(FP8X4),
-                scales=feature_rows[job][2].rearrange("p c t -> p (c t)"),
-                in_=grouped_rows[job][:].rearrange("p c t u -> p (c t u)").bitcast(BF16),
+                out=job[3].rearrange("p c t -> p (c t)").bitcast(FP8X4),
+                scales=job[4].rearrange("p c t -> p (c t)"),
+                in_=grouped_rows[job[0:2]][:].rearrange("p c t u -> p (c t u)").bitcast(BF16),
             )
-
-        pipeline(len(feature_rows), [flip_rows, group_rows, quantise_rows])
 
         v_codes = keep.tile([P, WINDOWS, HEADS, HEAD_DIM], U32, align_bytes=64)
         v_scales = keep.tile([P, WINDOWS, HEADS, HEAD_DIM], U8, align_bytes=64)
@@ -131,8 +125,8 @@ def tile_hybridattention_pa_kernel(tc, x, Wv, q, k, out):
         v_grouped = {}
 
         def project(job):
-            w, h = divmod(job, HEADS)
-            sums = psum_mx.tile([P, PACK, HEAD_DIM], F32, tag="mx")
+            w, h = job
+            sums = psum_work.tile([P, PACK, HEAD_DIM], F32, tag="work")
             for j in range(PACK):
                 for c in range(FEATURE_PASSES):
                     nc.tensor.matmul_mx(
@@ -152,52 +146,66 @@ def tile_hybridattention_pa_kernel(tc, x, Wv, q, k, out):
             v_grouped[job] = grouped
 
         def quantise_v(job):
-            w, h = divmod(job, HEADS)
+            w, h = job
             nc.vector.quantize_mx(
                 out=v_codes[:, w, h, :].bitcast(FP8X4),
                 scales=v_scales[:, w, h, :],
                 in_=v_grouped[job][:].rearrange("p d j -> p (d j)"),
             )
 
-        pipeline(WINDOWS * HEADS, [project, group_v, quantise_v])
-
         kT = keep.tile([P, HEADS, SEQ], BF16)
         qT = keep.tile([P, HEADS, WINDOWS, TILES_PER_WINDOW, P], BF16)
-        head_rows = [
-            (k_raw[:, h, TILES_PER_WINDOW * w : TILES_PER_WINDOW * (w + 1), :],
-             kT[:, h, WINDOW * w : WINDOW * (w + 1)])
-            for h in range(HEADS)
-            for w in range(WINDOWS)
-        ]
-        head_rows += [
-            (q_raw[:, h, w], qT[:, h, w].rearrange("d r p -> d (r p)"))
-            for h in range(HEADS)
-            for w in range(WINDOWS)
-        ]
         flipped_heads = {}
 
+        def k_job(h, w):
+            tiles = k_raw[:, h, TILES_PER_WINDOW * w : TILES_PER_WINDOW * (w + 1), :]
+            return ("k", h, w, tiles, kT[:, h, WINDOW * w : WINDOW * (w + 1)])
+
+        def q_job(h, w):
+            return ("q", h, w, q_raw[:, h, w], qT[:, h, w].rearrange("d r p -> d (r p)"))
+
         def flip_heads(job):
-            flipped = psum_plain.tile([P, TILES_PER_WINDOW, P], BF16, tag="plain")
+            flipped = psum_work.tile([P, TILES_PER_WINDOW, P], BF16, tag="work")
             for a in range(TILES_PER_WINDOW):
-                nc.tensor.transpose(flipped[:, a, :], head_rows[job][0][:, a, :], ident_bf16[:])
-            flipped_heads[job] = flipped
+                nc.tensor.transpose(flipped[:, a, :], job[3][:, a, :], ident_bf16[:])
+            flipped_heads[job[0:3]] = flipped
 
         def keep_heads(job):
             nc.vector.tensor_copy(
-                out=head_rows[job][1], in_=flipped_heads[job][:].rearrange("d a p -> d (a p)")
+                out=job[4], in_=flipped_heads[job[0:3]][:].rearrange("d a p -> d (a p)")
             )
 
-        pipeline(len(head_rows), [flip_heads, keep_heads])
+        rows_stages = (flip_rows, group_rows, quantise_rows)
+        head_stages = (flip_heads, keep_heads)
+        value_stages = (project, group_v, quantise_v)
+        preparation = []
+        for h in range(HEADS):
+            preparation.append((rows_stages, w_jobs[h]))
+            for w in range(WINDOWS):
+                preparation.append((head_stages, k_job(h, w)))
+                preparation.append((head_stages, q_job(h, w)))
+            if h == 0:
+                for n in range(ROW_TILES):
+                    preparation.append((rows_stages, x_jobs[n]))
+                lead = len(preparation)
+            for w in range(WINDOWS):
+                preparation.append((value_stages, (w, h)))
+
+        def prepare(position, lag):
+            if 0 <= position - lag < len(preparation):
+                stages, job = preparation[position - lag]
+                if lag < len(stages):
+                    stages[lag](job)
 
         units = [
-            (w, r, h)
-            for w in range(WINDOWS)
-            for r in range(TILES_PER_WINDOW)
+            (h, w, r)
             for h in range(HEADS)
+            for w in WINDOW_ORDER
+            for r in range(TILES_PER_WINDOW)
         ]
 
         def key_windows(unit):
-            w = units[unit][0]
+            w = units[unit][1]
             return [0] if w == 0 else [0, w]
 
         score_banks = {}
@@ -212,13 +220,12 @@ def tile_hybridattention_pa_kernel(tc, x, Wv, q, k, out):
         products = {}
         totals = {}
         inverses = {}
-        results = {}
 
         def scores(unit):
-            w, r, h = units[unit]
+            h, w, r = units[unit]
             score_banks[unit] = []
             for kw in key_windows(unit):
-                bank = psum_plain.tile([P, WINDOW], F32, tag="plain")
+                bank = psum_scores.tile([P, WINDOW], F32, tag="scores")
                 nc.tensor.matmul(
                     out=bank[:],
                     lhsT=qT[:, h, w, r, :],
@@ -249,9 +256,9 @@ def tile_hybridattention_pa_kernel(tc, x, Wv, q, k, out):
             bias_of[unit] = bias
 
         def exponentials(unit):
-            group, slot = divmod(unit, HEADS_PER_BANK)
+            group, slot = divmod(unit, TILES_PER_WINDOW)
             if slot == 0:
-                sums = small.tile([P, HEADS_PER_BANK, 2], F32, tag="row_sums")
+                sums = small.tile([P, TILES_PER_WINDOW, 2], F32, tag="row_sums")
                 row_sums[group] = sums
             bias = bias_of[unit]
             e = stage.tile([P, 2 * WINDOW], BF16, tag="e")
@@ -268,7 +275,7 @@ def tile_hybridattention_pa_kernel(tc, x, Wv, q, k, out):
 
         def flip_e(unit):
             words = e_of[unit][:].bitcast(F32)
-            flipped = psum_flip.tile([P, 2, 2, P], F32, tag="flip")
+            flipped = psum_work.tile([P, 2, 2, P], F32, tag="work")
             for g in range(len(key_windows(unit))):
                 for u in range(2):
                     slab = 2 * g + u
@@ -299,10 +306,10 @@ def tile_hybridattention_pa_kernel(tc, x, Wv, q, k, out):
             e_scales[unit] = scales
 
         def multiply(unit):
-            h = units[unit][2]
-            group, slot = divmod(unit, HEADS_PER_BANK)
+            h = units[unit][0]
+            group, slot = divmod(unit, TILES_PER_WINDOW)
             if slot == 0:
-                sums = psum_mx.tile([P, HEADS_PER_BANK, HEAD_DIM], F32, tag="mx")
+                sums = psum_work.tile([P, TILES_PER_WINDOW, HEAD_DIM], F32, tag="work")
                 products[group] = sums
             codes = e_codes[unit]
             scales = e_scales[unit]
@@ -319,45 +326,43 @@ def tile_hybridattention_pa_kernel(tc, x, Wv, q, k, out):
                 )
 
         def add_row_sums(group):
-            groups = len(key_windows(group * HEADS_PER_BANK))
-            total = small.tile([P, HEADS_PER_BANK], F32, tag="total")
+            groups = len(key_windows(group * TILES_PER_WINDOW))
+            total = small.tile([P, TILES_PER_WINDOW], F32, tag="total")
             nc.vector.tensor_reduce(
                 out=total[:], in_=row_sums[group][:, :, 0:groups], axis=AXIS_X, op=ALU.add
             )
             totals[group] = total
 
         def invert_row_sums(group):
-            inverse = small.tile([P, HEADS_PER_BANK], F32, tag="inverse")
+            inverse = small.tile([P, TILES_PER_WINDOW], F32, tag="inverse")
             nc.vector.reciprocal(out=inverse[:], in_=totals[group][:])
             inverses[group] = inverse
 
         def normalise(group):
-            w, r, h = units[group * HEADS_PER_BANK]
-            if h == 0:
-                result = stage.tile([P, HEADS, HEAD_DIM], F32, tag="result")
-                results[(w, r)] = result
+            h, w, r = units[group * TILES_PER_WINDOW]
+            result = stage.tile([P, TILES_PER_WINDOW, HEAD_DIM], F32, tag="result")
             nc.vector.tensor_tensor(
-                out=results[(w, r)][:, h : h + HEADS_PER_BANK, :],
+                out=result[:],
                 in0=products[group][:],
-                in1=inverses[group][:].unsqueeze(2).to_broadcast([P, HEADS_PER_BANK, HEAD_DIM]),
+                in1=inverses[group][:].unsqueeze(2).to_broadcast([P, TILES_PER_WINDOW, HEAD_DIM]),
                 op=ALU.mult,
             )
-            if h + HEADS_PER_BANK == HEADS:
-                window_rows = out_rows[WINDOW * w : WINDOW * (w + 1), :]
-                nc.sync.dma_start(
-                    out=window_rows.rearrange("(p r) n -> p r n", r=TILES_PER_WINDOW)[:, r, :],
-                    in_=results[(w, r)][:].rearrange("p h d -> p (h d)"),
-                )
+            nc.sync.dma_start(
+                out=out_rows[
+                    WINDOW * w : WINDOW * (w + 1), HEAD_DIM * h : HEAD_DIM * (h + 1)
+                ].rearrange("(p r) d -> p r d", r=TILES_PER_WINDOW),
+                in_=result[:],
+            )
 
         def for_unit(stage_fn, unit):
             if 0 <= unit < len(units):
                 stage_fn(unit)
 
         def for_group(stage_fn, unit):
-            if 0 <= unit < len(units) and unit % HEADS_PER_BANK == HEADS_PER_BANK - 1:
-                stage_fn(unit // HEADS_PER_BANK)
+            if 0 <= unit < len(units) and unit % TILES_PER_WINDOW == TILES_PER_WINDOW - 1:
+                stage_fn(unit // TILES_PER_WINDOW)
 
-        for step in range(len(units) + 7):
+        for step in range(-lead, len(units) + 7):
             for_unit(exponentials, step - 2)
             for_unit(scores, step)
             for_unit(flip_e, step - 2)
@@ -367,5 +372,8 @@ def tile_hybridattention_pa_kernel(tc, x, Wv, q, k, out):
             for_unit(quantise_e, step - 4)
             for_unit(exp_bias, step - 1)
             for_group(invert_row_sums, step - 4)
+            prepare(step + lead, 0)
             for_unit(multiply, step - 5)
             for_group(normalise, step - 6)
+            prepare(step + lead, 1)
+            prepare(step + lead, 2)

@@ -25,7 +25,6 @@ ROW_TILES = SEQ // P
 TILES_PER_WINDOW = WINDOW // P
 FEATURE_PASSES = FEATURES // K_PASS
 WORD_SLABS = FEATURES // (2 * P)
-WINDOW_ORDER = (1, 2, 0)
 SCALE = HEAD_DIM**-0.5
 
 FLOPS = 2 * SEQ * FEATURES * FEATURES + 2 * (2 * HEADS * SEQ * 2 * WINDOW * HEAD_DIM)
@@ -197,34 +196,33 @@ def tile_hybridattention_pa_kernel(tc, x, Wv, q, k, out):
                 if lag < len(stages):
                     stages[lag](job)
 
-        units = [
-            (h, w, r)
-            for h in range(HEADS)
-            for w in WINDOW_ORDER
-            for r in range(TILES_PER_WINDOW)
-        ]
-
-        def key_windows(unit):
-            w = units[unit][1]
-            return [0] if w == 0 else [0, w]
+        units = []
+        for h in range(HEADS):
+            for w in range(WINDOWS):
+                if w == 0:
+                    for r in range(0, TILES_PER_WINDOW, 2):
+                        units.append((h, w, [(r, 0), (r + 1, 0)]))
+                else:
+                    for r in range(TILES_PER_WINDOW):
+                        units.append((h, w, [(r, 0), (r, w)]))
 
         score_banks = {}
         maxima_of = {}
         bias_of = {}
-        row_sums = {}
         e_of = {}
         flipped_e = {}
         grouped_e = {}
         e_codes = {}
         e_scales = {}
-        products = {}
+        row_sums = {}
         totals = {}
         inverses = {}
+        products = {}
 
         def scores(unit):
-            h, w, r = units[unit]
+            h, w, halves = units[unit]
             score_banks[unit] = []
-            for kw in key_windows(unit):
+            for r, kw in halves:
                 bank = psum_scores.tile([P, WINDOW], F32, tag="scores")
                 nc.tensor.matmul(
                     out=bank[:],
@@ -242,41 +240,48 @@ def tile_hybridattention_pa_kernel(tc, x, Wv, q, k, out):
             maxima_of[unit] = maxima
 
         def exp_bias(unit):
+            w = units[unit][1]
             maxima = maxima_of[unit]
-            last = len(score_banks[unit]) - 1
-            bias = small.tile([P, 1], F32, tag="bias")
-            nc.vector.tensor_scalar(
-                out=bias[:],
-                in0=maxima[:, 0:1],
-                scalar1=maxima[:, last : last + 1],
-                scalar2=-SCALE,
-                op0=ALU.max,
-                op1=ALU.mult,
-            )
+            bias = small.tile([P, 2], F32, tag="bias")
+            if w == 0:
+                nc.gpsimd.tensor_scalar(
+                    out=bias[:], in0=maxima[:], scalar1=-SCALE, scalar2=0.0, op0=ALU.mult, op1=ALU.add
+                )
+            else:
+                nc.gpsimd.tensor_scalar(
+                    out=bias[:, 0:1],
+                    in0=maxima[:, 0:1],
+                    scalar1=maxima[:, 1:2],
+                    scalar2=-SCALE,
+                    op0=ALU.max,
+                    op1=ALU.mult,
+                )
             bias_of[unit] = bias
 
         def exponentials(unit):
-            group, slot = divmod(unit, TILES_PER_WINDOW)
-            if slot == 0:
+            h, w, halves = units[unit]
+            if halves[0][0] == 0:
                 sums = small.tile([P, TILES_PER_WINDOW, 2], F32, tag="row_sums")
-                row_sums[group] = sums
-            bias = bias_of[unit]
+                row_sums[(h, w)] = sums
             e = stage.tile([P, 2 * WINDOW], BF16, tag="e")
             for g, bank in enumerate(score_banks[unit]):
+                column = g if w == 0 else 0
+                part = 0 if w == 0 else g
+                r = halves[g][0]
                 nc.scalar.activation(
                     out=e[:, WINDOW * g : WINDOW * (g + 1)],
                     in_=bank[:],
                     func=EXP,
-                    bias=bias[:],
+                    bias=bias_of[unit][:, column : column + 1],
                     scale=SCALE,
-                    accum_out=row_sums[group][:, slot, g : g + 1],
+                    accum_out=row_sums[(h, w)][:, r, part : part + 1],
                 )
             e_of[unit] = e
 
         def flip_e(unit):
             words = e_of[unit][:].bitcast(F32)
             flipped = psum_work.tile([P, 2, 2, P], F32, tag="work")
-            for g in range(len(key_windows(unit))):
+            for g in range(2):
                 for u in range(2):
                     slab = 2 * g + u
                     nc.tensor.transpose(
@@ -285,61 +290,53 @@ def tile_hybridattention_pa_kernel(tc, x, Wv, q, k, out):
             flipped_e[unit] = flipped
 
         def group_e(unit):
-            groups = len(key_windows(unit))
             grouped = stage.tile([P, 2, P, 2], F32, tag="grouped_e", align_bytes=64)
-            nc.scalar.copy(
-                out=grouped[:, 0:groups],
-                in_=flipped_e[unit][:, 0:groups].rearrange("p g u q -> p g q u"),
-            )
+            nc.scalar.copy(out=grouped[:], in_=flipped_e[unit][:].rearrange("p g u q -> p g q u"))
             grouped_e[unit] = grouped
 
         def quantise_e(unit):
-            groups = len(key_windows(unit))
-            codes = stage.tile([P, 2 * P], U32, tag="e_codes", align_bytes=64)
-            scales = stage.tile([P, 2 * P], U8, tag="e_scales", align_bytes=64)
+            codes = stage.tile([P, 2, P], U32, tag="e_codes", align_bytes=64)
+            scales = stage.tile([P, 2, P], U8, tag="e_scales", align_bytes=64)
             nc.vector.quantize_mx(
-                out=codes[:, 0 : groups * P].bitcast(FP8X4),
-                scales=scales[:, 0 : groups * P],
-                in_=grouped_e[unit][:, 0:groups].rearrange("p g q u -> p (g q u)").bitcast(BF16),
+                out=codes[:].rearrange("p g q -> p (g q)").bitcast(FP8X4),
+                scales=scales[:].rearrange("p g q -> p (g q)"),
+                in_=grouped_e[unit][:].rearrange("p g q u -> p (g q u)").bitcast(BF16),
             )
             e_codes[unit] = codes
             e_scales[unit] = scales
 
         def multiply(unit):
-            h = units[unit][0]
-            group, slot = divmod(unit, TILES_PER_WINDOW)
-            if slot == 0:
+            h, w, halves = units[unit]
+            if halves[0][0] == 0:
                 sums = psum_work.tile([P, TILES_PER_WINDOW, HEAD_DIM], F32, tag="work")
-                products[group] = sums
-            codes = e_codes[unit]
-            scales = e_scales[unit]
-            windows = key_windows(unit)
-            for g, kw in enumerate(windows):
+                products[(h, w)] = sums
+            for g, (r, kw) in enumerate(halves):
                 nc.tensor.matmul_mx(
-                    out=products[group][:, slot, :],
-                    lhsT=codes[:, g * P : (g + 1) * P].bitcast(FP8X4),
-                    lhsT_scale=scales[:, g * P : (g + 1) * P],
+                    out=products[(h, w)][:, r, :],
+                    lhsT=e_codes[unit][:, g, :].bitcast(FP8X4),
+                    lhsT_scale=e_scales[unit][:, g, :],
                     rhs=v_codes[:, kw, h, :].bitcast(FP8X4),
                     rhs_scale=v_scales[:, kw, h, :],
-                    start=(g == 0),
-                    stop=(g == len(windows) - 1),
+                    start=(w == 0 or g == 0),
+                    stop=(w == 0 or g == 1),
                 )
 
         def add_row_sums(group):
-            groups = len(key_windows(group * TILES_PER_WINDOW))
-            total = small.tile([P, TILES_PER_WINDOW], F32, tag="total")
-            nc.vector.tensor_reduce(
-                out=total[:], in_=row_sums[group][:, :, 0:groups], axis=AXIS_X, op=ALU.add
-            )
-            totals[group] = total
+            sums = row_sums[group]
+            if group[1] == 0:
+                totals[group] = sums[:, :, 0]
+            else:
+                total = small.tile([P, TILES_PER_WINDOW], F32, tag="total")
+                nc.gpsimd.tensor_tensor(out=total[:], in0=sums[:, :, 0], in1=sums[:, :, 1], op=ALU.add)
+                totals[group] = total[:]
 
         def invert_row_sums(group):
             inverse = small.tile([P, TILES_PER_WINDOW], F32, tag="inverse")
-            nc.vector.reciprocal(out=inverse[:], in_=totals[group][:])
+            nc.vector.reciprocal(out=inverse[:], in_=totals[group])
             inverses[group] = inverse
 
         def normalise(group):
-            h, w, r = units[group * TILES_PER_WINDOW]
+            h, w = group
             result = stage.tile([P, TILES_PER_WINDOW, HEAD_DIM], F32, tag="result")
             nc.vector.tensor_tensor(
                 out=result[:],
@@ -359,8 +356,10 @@ def tile_hybridattention_pa_kernel(tc, x, Wv, q, k, out):
                 stage_fn(unit)
 
         def for_group(stage_fn, unit):
-            if 0 <= unit < len(units) and unit % TILES_PER_WINDOW == TILES_PER_WINDOW - 1:
-                stage_fn(unit // TILES_PER_WINDOW)
+            if 0 <= unit < len(units):
+                h, w, halves = units[unit]
+                if halves[1][0] == TILES_PER_WINDOW - 1:
+                    stage_fn((h, w))
 
         for step in range(-lead, len(units) + 7):
             for_unit(exponentials, step - 2)
@@ -368,9 +367,9 @@ def tile_hybridattention_pa_kernel(tc, x, Wv, q, k, out):
             for_unit(flip_e, step - 2)
             for_unit(group_e, step - 3)
             for_unit(row_maxima, step - 1)
+            for_unit(exp_bias, step - 1)
             for_group(add_row_sums, step - 3)
             for_unit(quantise_e, step - 4)
-            for_unit(exp_bias, step - 1)
             for_group(invert_row_sums, step - 4)
             prepare(step + lead, 0)
             for_unit(multiply, step - 5)

@@ -38,7 +38,6 @@ def tile_hybridattention_pa_kernel(tc, x, Wv, q, k, out):
     k_heads = k.rearrange("b h t d -> (b h) t d")
 
     with ExitStack() as stack:
-        stack.enter_context(tc.manual_schedule())
         keep = stack.enter_context(tc.tile_pool(name="keep", bufs=1))
         stage = stack.enter_context(tc.tile_pool(name="stage", bufs=3))
         small = stack.enter_context(tc.tile_pool(name="small", bufs=4))

@@ -14,6 +14,8 @@ AXIS_X = mybir.AxisListType.X
 
 P = 128
 PACK = 4
+WORD = 2
+PAIRS = PACK // WORD
 K_PASS = P * PACK
 HEADS = 8
 HEAD_DIM = 128
@@ -24,8 +26,16 @@ WINDOWS = SEQ // WINDOW
 ROW_TILES = SEQ // P
 TILES_PER_WINDOW = WINDOW // P
 FEATURE_PASSES = FEATURES // K_PASS
-WORD_SLABS = FEATURES // (2 * P)
+WORD_SLABS = FEATURES // (WORD * P)
+HALVES = 2
 SCALE = HEAD_DIM**-0.5
+
+MAXIMA_LAG = 1
+EXP_LAG = 2
+REGROUP_LAG = 3
+QUANTISE_LAG = 4
+PRODUCT_LAG = 5
+DIVIDE_LAG = 6
 
 FLOPS = 2 * SEQ * FEATURES * FEATURES + 2 * (2 * HEADS * SEQ * 2 * WINDOW * HEAD_DIM)
 
@@ -47,12 +57,10 @@ def tile_hybridattention_pa_kernel(tc, x, Wv, q, k, out):
         w_raw = keep.tile([P, HEADS, FEATURES], BF16)
         k_raw = keep.tile([P, HEADS, ROW_TILES, HEAD_DIM], BF16)
         q_raw = keep.tile([P, HEADS, WINDOWS, TILES_PER_WINDOW, HEAD_DIM], BF16)
-        x_raw = keep.tile([P, ROW_TILES // 2, 2, FEATURES], BF16)
+        x_raw = keep.tile([P, ROW_TILES // WORD, WORD, FEATURES], BF16)
         for h in range(HEADS):
             nc.sync.dma_start(out=w_raw[:, h, :], in_=Wv[P * h : P * (h + 1), :])
-            nc.sync.dma_start(
-                out=k_raw[:, h], in_=k_heads[h].rearrange("(a p) d -> p a d", p=P)
-            )
+            nc.sync.dma_start(out=k_raw[:, h], in_=k_heads[h].rearrange("(a p) d -> p a d", p=P))
             nc.sync.dma_start(
                 out=q_raw[:, h].rearrange("p w r d -> p w (r d)"),
                 in_=q_heads[h].rearrange(
@@ -60,11 +68,11 @@ def tile_hybridattention_pa_kernel(tc, x, Wv, q, k, out):
                 ),
             )
             if h == 0:
-                for c in range(ROW_TILES // 2):
+                for c in range(ROW_TILES // WORD):
                     nc.sync.dma_start(
                         out=x_raw[:, c],
-                        in_=x_rows[2 * P * c : 2 * P * (c + 1), :].rearrange(
-                            "(p e) i -> p e i", e=2
+                        in_=x_rows[WORD * P * c : WORD * P * (c + 1), :].rearrange(
+                            "(p e) i -> p e i", e=WORD
                         ),
                     )
 
@@ -78,147 +86,154 @@ def tile_hybridattention_pa_kernel(tc, x, Wv, q, k, out):
         one = keep.tile([P, 1], F32)
         nc.scalar.activation(out=one[:], in_=zero[:], func=EXP)
 
+
         w_codes = keep.tile([P, HEADS, FEATURE_PASSES, P], U32, align_bytes=64)
         w_scales = keep.tile([P, HEADS, FEATURE_PASSES, P], U8, align_bytes=64)
         x_codes = keep.tile([P, ROW_TILES, FEATURE_PASSES, P], U32, align_bytes=64)
         x_scales = keep.tile([P, ROW_TILES, FEATURE_PASSES, P], U8, align_bytes=64)
-        w_jobs = [
-            ("w", h, w_raw[:, h, :], w_codes[:, h], w_scales[:, h], nc.vector.tensor_copy)
-            for h in range(HEADS)
-        ]
-        x_jobs = [
-            ("x", n, x_raw[:, n // 2, n % 2, :], x_codes[:, n], x_scales[:, n], nc.scalar.copy)
-            for n in range(ROW_TILES)
-        ]
-        flipped_rows = {}
-        grouped_rows = {}
 
-        def flip_rows(job):
-            words = job[2].bitcast(F32)
-            flipped = psum_work.tile([P, WORD_SLABS, P], F32, tag="work")
-            for slab in range(WORD_SLABS):
-                nc.tensor.transpose(
-                    flipped[:, slab, :], words[:, slab * P : (slab + 1) * P], ident_f32[:]
+        def rows_entry(rows, codes, scales, copy_out):
+            tiles = {}
+
+            def transpose_rows():
+                words = rows.bitcast(F32)
+                transposed = psum_work.tile([P, WORD_SLABS, P], F32, tag="work")
+                for slab in range(WORD_SLABS):
+                    nc.tensor.transpose(
+                        transposed[:, slab, :], words[:, slab * P : (slab + 1) * P], ident_f32[:]
+                    )
+                tiles["transposed"] = transposed
+
+            def regroup_rows():
+                regrouped = stage.tile([P, FEATURE_PASSES, P, PAIRS], F32, tag="rows", align_bytes=64)
+                copy_out(
+                    out=regrouped[:],
+                    in_=tiles["transposed"][:].rearrange("p (c u) t -> p c t u", u=PAIRS),
                 )
-            flipped_rows[job[0:2]] = flipped
+                tiles["regrouped"] = regrouped
 
-        def group_rows(job):
-            grouped = stage.tile([P, FEATURE_PASSES, P, 2], F32, tag="grouped_rows", align_bytes=64)
-            job[5](
-                out=grouped[:],
-                in_=flipped_rows[job[0:2]][:].rearrange("p (c u) t -> p c t u", u=2),
-            )
-            grouped_rows[job[0:2]] = grouped
+            def quantise_rows():
+                nc.vector.quantize_mx(
+                    out=codes.rearrange("p c t -> p (c t)").bitcast(FP8X4),
+                    scales=scales.rearrange("p c t -> p (c t)"),
+                    in_=tiles["regrouped"][:].rearrange("p c t u -> p (c t u)").bitcast(BF16),
+                )
 
-        def quantise_rows(job):
-            nc.vector.quantize_mx(
-                out=job[3].rearrange("p c t -> p (c t)").bitcast(FP8X4),
-                scales=job[4].rearrange("p c t -> p (c t)"),
-                in_=grouped_rows[job[0:2]][:].rearrange("p c t u -> p (c t u)").bitcast(BF16),
-            )
+            return (transpose_rows, regroup_rows, quantise_rows)
 
         v_codes = keep.tile([P, WINDOWS, HEADS, HEAD_DIM], U32, align_bytes=64)
         v_scales = keep.tile([P, WINDOWS, HEADS, HEAD_DIM], U8, align_bytes=64)
-        v_sums = {}
-        v_grouped = {}
 
-        def project(job):
-            w, h = job
-            sums = psum_work.tile([P, PACK, HEAD_DIM], F32, tag="work")
-            for j in range(PACK):
-                for c in range(FEATURE_PASSES):
-                    nc.tensor.matmul_mx(
-                        out=sums[:, j, :],
-                        lhsT=x_codes[:, PACK * w + j, c, :].bitcast(FP8X4),
-                        lhsT_scale=x_scales[:, PACK * w + j, c, :],
-                        rhs=w_codes[:, h, c, :].bitcast(FP8X4),
-                        rhs_scale=w_scales[:, h, c, :],
-                        start=(c == 0),
-                        stop=(c == FEATURE_PASSES - 1),
-                    )
-            v_sums[job] = sums
+        def values_entry(w, h):
+            tiles = {}
 
-        def group_v(job):
-            grouped = stage.tile([P, HEAD_DIM, PACK], BF16, tag="v_grouped", align_bytes=64)
-            nc.scalar.copy(out=grouped[:], in_=v_sums[job][:].rearrange("p j d -> p d j"))
-            v_grouped[job] = grouped
+            def project():
+                projected = psum_work.tile([P, PACK, HEAD_DIM], F32, tag="work")
+                for j in range(PACK):
+                    for c in range(FEATURE_PASSES):
+                        nc.tensor.matmul_mx(
+                            out=projected[:, j, :],
+                            lhsT=x_codes[:, PACK * w + j, c, :].bitcast(FP8X4),
+                            lhsT_scale=x_scales[:, PACK * w + j, c, :],
+                            rhs=w_codes[:, h, c, :].bitcast(FP8X4),
+                            rhs_scale=w_scales[:, h, c, :],
+                            start=(c == 0),
+                            stop=(c == FEATURE_PASSES - 1),
+                        )
+                tiles["projected"] = projected
 
-        def quantise_v(job):
-            w, h = job
-            nc.vector.quantize_mx(
-                out=v_codes[:, w, h, :].bitcast(FP8X4),
-                scales=v_scales[:, w, h, :],
-                in_=v_grouped[job][:].rearrange("p d j -> p (d j)"),
-            )
+            def regroup_values():
+                regrouped = stage.tile([P, HEAD_DIM, PACK], BF16, tag="values", align_bytes=64)
+                nc.scalar.copy(
+                    out=regrouped[:], in_=tiles["projected"][:].rearrange("p j d -> p d j")
+                )
+                tiles["regrouped"] = regrouped
+
+            def quantise_values():
+                nc.vector.quantize_mx(
+                    out=v_codes[:, w, h, :].bitcast(FP8X4),
+                    scales=v_scales[:, w, h, :],
+                    in_=tiles["regrouped"][:].rearrange("p d j -> p (d j)"),
+                )
+
+            return (project, regroup_values, quantise_values)
 
         kT = keep.tile([P, HEADS, SEQ], BF16)
         qT = keep.tile([P, HEADS, WINDOWS, TILES_PER_WINDOW, P], BF16)
-        flipped_heads = {}
 
-        def k_job(h, w):
-            tiles = k_raw[:, h, TILES_PER_WINDOW * w : TILES_PER_WINDOW * (w + 1), :]
-            return ("k", h, w, tiles, kT[:, h, WINDOW * w : WINDOW * (w + 1)])
+        def head_entry(row_tiles, place):
+            tiles = {}
 
-        def q_job(h, w):
-            return ("q", h, w, q_raw[:, h, w], qT[:, h, w].rearrange("d r p -> d (r p)"))
+            def transpose_head():
+                transposed = psum_work.tile([P, TILES_PER_WINDOW, P], BF16, tag="work")
+                for a in range(TILES_PER_WINDOW):
+                    nc.tensor.transpose(transposed[:, a, :], row_tiles[:, a, :], ident_bf16[:])
+                tiles["transposed"] = transposed
 
-        def flip_heads(job):
-            flipped = psum_work.tile([P, TILES_PER_WINDOW, P], BF16, tag="work")
-            for a in range(TILES_PER_WINDOW):
-                nc.tensor.transpose(flipped[:, a, :], job[3][:, a, :], ident_bf16[:])
-            flipped_heads[job[0:3]] = flipped
+            def keep_head():
+                nc.vector.tensor_copy(
+                    out=place, in_=tiles["transposed"][:].rearrange("d a p -> d (a p)")
+                )
 
-        def keep_heads(job):
-            nc.vector.tensor_copy(
-                out=job[4], in_=flipped_heads[job[0:3]][:].rearrange("d a p -> d (a p)")
-            )
+            return (transpose_head, keep_head)
 
-        rows_stages = (flip_rows, group_rows, quantise_rows)
-        head_stages = (flip_heads, keep_heads)
-        value_stages = (project, group_v, quantise_v)
         preparation = []
         for h in range(HEADS):
-            preparation.append((rows_stages, w_jobs[h]))
+            preparation.append(
+                rows_entry(w_raw[:, h, :], w_codes[:, h], w_scales[:, h], nc.vector.tensor_copy)
+            )
             for w in range(WINDOWS):
-                preparation.append((head_stages, k_job(h, w)))
-                preparation.append((head_stages, q_job(h, w)))
+                first_tile = TILES_PER_WINDOW * w
+                preparation.append(
+                    head_entry(
+                        k_raw[:, h, first_tile : first_tile + TILES_PER_WINDOW, :],
+                        kT[:, h, WINDOW * w : WINDOW * (w + 1)],
+                    )
+                )
+                preparation.append(
+                    head_entry(q_raw[:, h, w], qT[:, h, w].rearrange("d r p -> d (r p)"))
+                )
             if h == 0:
                 for n in range(ROW_TILES):
-                    preparation.append((rows_stages, x_jobs[n]))
+                    preparation.append(
+                        rows_entry(
+                            x_raw[:, n // WORD, n % WORD, :], x_codes[:, n], x_scales[:, n], nc.scalar.copy
+                        )
+                    )
                 lead = len(preparation)
             for w in range(WINDOWS):
-                preparation.append((value_stages, (w, h)))
+                preparation.append(values_entry(w, h))
 
         def prepare(position, lag):
             if 0 <= position - lag < len(preparation):
-                stages, job = preparation[position - lag]
+                stages = preparation[position - lag]
                 if lag < len(stages):
-                    stages[lag](job)
+                    stages[lag]()
 
         units = []
         for h in range(HEADS):
             for w in range(WINDOWS):
                 if w == 0:
-                    for r in range(0, TILES_PER_WINDOW, 2):
+                    for r in range(0, TILES_PER_WINDOW, HALVES):
                         units.append((h, w, [(r, 0), (r + 1, 0)]))
                 else:
                     for r in range(TILES_PER_WINDOW):
                         units.append((h, w, [(r, 0), (r, w)]))
 
         score_banks = {}
-        maxima_of = {}
-        bias_of = {}
-        e_of = {}
-        flipped_e = {}
-        grouped_e = {}
+        row_maxima = {}
+        exp_biases = {}
+        exponentials = {}
+        transposed_e = {}
+        regrouped_e = {}
         e_codes = {}
         e_scales = {}
         row_sums = {}
-        totals = {}
+        denominators = {}
         inverses = {}
         products = {}
 
-        def scores(unit):
+        def compute_scores(unit):
             h, w, halves = units[unit]
             score_banks[unit] = []
             for r, kw in halves:
@@ -232,16 +247,18 @@ def tile_hybridattention_pa_kernel(tc, x, Wv, q, k, out):
                 )
                 score_banks[unit].append(bank)
 
-        def row_maxima(unit):
-            maxima = small.tile([P, 2], F32, tag="maxima")
+        def find_maxima(unit):
+            maxima = small.tile([P, HALVES], F32, tag="maxima")
             for g, bank in enumerate(score_banks[unit]):
-                nc.vector.tensor_reduce(out=maxima[:, g : g + 1], in_=bank[:], axis=AXIS_X, op=ALU.max)
-            maxima_of[unit] = maxima
+                nc.vector.tensor_reduce(
+                    out=maxima[:, g : g + 1], in_=bank[:], axis=AXIS_X, op=ALU.max
+                )
+            row_maxima[unit] = maxima
 
-        def exp_bias(unit):
+        def make_bias(unit):
             w = units[unit][1]
-            maxima = maxima_of[unit]
-            bias = small.tile([P, 2], F32, tag="bias")
+            maxima = row_maxima[unit]
+            bias = small.tile([P, HALVES], F32, tag="bias")
             if w == 0:
                 nc.gpsimd.tensor_scalar(
                     out=bias[:], in0=maxima[:], scalar1=-SCALE, scalar2=0.0, op0=ALU.mult, op1=ALU.add
@@ -255,60 +272,62 @@ def tile_hybridattention_pa_kernel(tc, x, Wv, q, k, out):
                     op0=ALU.max,
                     op1=ALU.mult,
                 )
-            bias_of[unit] = bias
+            exp_biases[unit] = bias
 
-        def exponentials(unit):
+        def exponentiate(unit):
             h, w, halves = units[unit]
             if halves[0][0] == 0:
-                sums = small.tile([P, TILES_PER_WINDOW, 2], F32, tag="row_sums")
+                sums = small.tile([P, TILES_PER_WINDOW, HALVES], F32, tag="sums")
                 row_sums[(h, w)] = sums
-            e = stage.tile([P, 2 * WINDOW], BF16, tag="e")
+            e = stage.tile([P, HALVES * WINDOW], BF16, tag="e")
             for g, bank in enumerate(score_banks[unit]):
-                column = g if w == 0 else 0
-                part = 0 if w == 0 else g
                 r = halves[g][0]
+                bias_column = g if w == 0 else 0
+                part = 0 if w == 0 else g
                 nc.scalar.activation(
                     out=e[:, WINDOW * g : WINDOW * (g + 1)],
                     in_=bank[:],
                     func=EXP,
-                    bias=bias_of[unit][:, column : column + 1],
+                    bias=exp_biases[unit][:, bias_column : bias_column + 1],
                     scale=SCALE,
                     accum_out=row_sums[(h, w)][:, r, part : part + 1],
                 )
-            e_of[unit] = e
+            exponentials[unit] = e
 
-        def flip_e(unit):
-            words = e_of[unit][:].bitcast(F32)
-            flipped = psum_work.tile([P, 2, 2, P], F32, tag="work")
-            for g in range(2):
-                for u in range(2):
-                    slab = 2 * g + u
+        def transpose_e(unit):
+            words = exponentials[unit][:].bitcast(F32)
+            transposed = psum_work.tile([P, HALVES, PAIRS, P], F32, tag="work")
+            for g in range(HALVES):
+                for u in range(PAIRS):
+                    slab = PAIRS * g + u
                     nc.tensor.transpose(
-                        flipped[:, g, u, :], words[:, slab * P : (slab + 1) * P], ident_f32[:]
+                        transposed[:, g, u, :], words[:, slab * P : (slab + 1) * P], ident_f32[:]
                     )
-            flipped_e[unit] = flipped
+            transposed_e[unit] = transposed
 
-        def group_e(unit):
-            grouped = stage.tile([P, 2, P, 2], F32, tag="grouped_e", align_bytes=64)
-            nc.scalar.copy(out=grouped[:], in_=flipped_e[unit][:].rearrange("p g u q -> p g q u"))
-            grouped_e[unit] = grouped
+        def regroup_e(unit):
+            regrouped = stage.tile([P, HALVES, P, PAIRS], F32, tag="regrouped_e", align_bytes=64)
+            nc.scalar.copy(
+                out=regrouped[:], in_=transposed_e[unit][:].rearrange("p g u q -> p g q u")
+            )
+            regrouped_e[unit] = regrouped
 
         def quantise_e(unit):
-            codes = stage.tile([P, 2, P], U32, tag="e_codes", align_bytes=64)
-            scales = stage.tile([P, 2, P], U8, tag="e_scales", align_bytes=64)
+            codes = stage.tile([P, HALVES, P], U32, tag="e_codes", align_bytes=64)
+            scales = stage.tile([P, HALVES, P], U8, tag="e_scales", align_bytes=64)
             nc.vector.quantize_mx(
                 out=codes[:].rearrange("p g q -> p (g q)").bitcast(FP8X4),
                 scales=scales[:].rearrange("p g q -> p (g q)"),
-                in_=grouped_e[unit][:].rearrange("p g q u -> p (g q u)").bitcast(BF16),
+                in_=regrouped_e[unit][:].rearrange("p g q u -> p (g q u)").bitcast(BF16),
             )
             e_codes[unit] = codes
             e_scales[unit] = scales
 
-        def multiply(unit):
+        def multiply_by_v(unit):
             h, w, halves = units[unit]
             if halves[0][0] == 0:
-                sums = psum_work.tile([P, TILES_PER_WINDOW, HEAD_DIM], F32, tag="work")
-                products[(h, w)] = sums
+                product = psum_work.tile([P, TILES_PER_WINDOW, HEAD_DIM], F32, tag="work")
+                products[(h, w)] = product
             for g, (r, kw) in enumerate(halves):
                 nc.tensor.matmul_mx(
                     out=products[(h, w)][:, r, :],
@@ -317,24 +336,26 @@ def tile_hybridattention_pa_kernel(tc, x, Wv, q, k, out):
                     rhs=v_codes[:, kw, h, :].bitcast(FP8X4),
                     rhs_scale=v_scales[:, kw, h, :],
                     start=(w == 0 or g == 0),
-                    stop=(w == 0 or g == 1),
+                    stop=(w == 0 or g == HALVES - 1),
                 )
 
         def add_row_sums(group):
             sums = row_sums[group]
             if group[1] == 0:
-                totals[group] = sums[:, :, 0]
+                denominators[group] = sums[:, :, 0]
             else:
                 total = small.tile([P, TILES_PER_WINDOW], F32, tag="total")
-                nc.gpsimd.tensor_tensor(out=total[:], in0=sums[:, :, 0], in1=sums[:, :, 1], op=ALU.add)
-                totals[group] = total[:]
+                nc.gpsimd.tensor_tensor(
+                    out=total[:], in0=sums[:, :, 0], in1=sums[:, :, 1], op=ALU.add
+                )
+                denominators[group] = total[:]
 
         def invert_row_sums(group):
             inverse = small.tile([P, TILES_PER_WINDOW], F32, tag="inverse")
-            nc.vector.reciprocal(out=inverse[:], in_=totals[group])
+            nc.vector.reciprocal(out=inverse[:], in_=denominators[group])
             inverses[group] = inverse
 
-        def normalise(group):
+        def divide_and_store(group):
             h, w = group
             result = stage.tile([P, TILES_PER_WINDOW, HEAD_DIM], F32, tag="result")
             nc.vector.tensor_tensor(
@@ -360,18 +381,18 @@ def tile_hybridattention_pa_kernel(tc, x, Wv, q, k, out):
                 if halves[1][0] == TILES_PER_WINDOW - 1:
                     stage_fn((h, w))
 
-        for step in range(-lead, len(units) + 7):
-            for_unit(exponentials, step - 2)
-            for_unit(scores, step)
-            for_unit(flip_e, step - 2)
-            for_unit(group_e, step - 3)
-            for_unit(row_maxima, step - 1)
-            for_unit(exp_bias, step - 1)
-            for_group(add_row_sums, step - 3)
-            for_unit(quantise_e, step - 4)
-            for_group(invert_row_sums, step - 4)
+        for step in range(-lead, len(units) + DIVIDE_LAG + 1):
+            for_unit(exponentiate, step - EXP_LAG)
+            for_unit(compute_scores, step)
+            for_unit(transpose_e, step - EXP_LAG)
+            for_unit(regroup_e, step - REGROUP_LAG)
+            for_unit(find_maxima, step - MAXIMA_LAG)
+            for_unit(make_bias, step - MAXIMA_LAG)
+            for_group(add_row_sums, step - REGROUP_LAG)
+            for_unit(quantise_e, step - QUANTISE_LAG)
+            for_group(invert_row_sums, step - QUANTISE_LAG)
             prepare(step + lead, 0)
-            for_unit(multiply, step - 5)
-            for_group(normalise, step - 6)
+            for_unit(multiply_by_v, step - PRODUCT_LAG)
+            for_group(divide_and_store, step - DIVIDE_LAG)
             prepare(step + lead, 1)
             prepare(step + lead, 2)

@@ -35,7 +35,8 @@ EXP_LAG = 2
 REGROUP_LAG = 3
 QUANTISE_LAG = 4
 PRODUCT_LAG = 5
-DIVIDE_LAG = 6
+LEAD = 2
+SPARE = 6
 
 FLOPS = 2 * SEQ * FEATURES * FEATURES + 2 * (2 * HEADS * SEQ * 2 * WINDOW * HEAD_DIM)
 
@@ -50,7 +51,8 @@ def tile_hybridattention_pa_kernel(tc, x, Wv, q, k, out):
     with ExitStack() as stack:
         keep = stack.enter_context(tc.tile_pool(name="keep", bufs=1))
         stage = stack.enter_context(tc.tile_pool(name="stage", bufs=3))
-        small = stack.enter_context(tc.tile_pool(name="small", bufs=4))
+        small = stack.enter_context(tc.tile_pool(name="small", bufs=8))
+        late = stack.enter_context(tc.tile_pool(name="late", bufs=14))
         psum_scores = stack.enter_context(tc.psum_pool(name="psum_scores", bufs=4))
         psum_work = stack.enter_context(tc.psum_pool(name="psum_work", bufs=4))
 
@@ -58,15 +60,25 @@ def tile_hybridattention_pa_kernel(tc, x, Wv, q, k, out):
         k_raw = keep.tile([P, HEADS, ROW_TILES, HEAD_DIM], BF16)
         q_raw = keep.tile([P, HEADS, WINDOWS, TILES_PER_WINDOW, HEAD_DIM], BF16)
         x_raw = keep.tile([P, ROW_TILES // WORD, WORD, FEATURES], BF16)
-        for h in range(HEADS):
-            nc.sync.dma_start(out=w_raw[:, h, :], in_=Wv[P * h : P * (h + 1), :])
-            nc.sync.dma_start(out=k_raw[:, h], in_=k_heads[h].rearrange("(a p) d -> p a d", p=P))
+        def load_keys_and_queries(h, first, last):
             nc.sync.dma_start(
-                out=q_raw[:, h].rearrange("p w r d -> p w (r d)"),
-                in_=q_heads[h].rearrange(
-                    "(w p r) d -> p w (r d)", w=WINDOWS, p=P, r=TILES_PER_WINDOW
+                out=k_raw[:, h, TILES_PER_WINDOW * first : TILES_PER_WINDOW * last, :],
+                in_=k_heads[h, WINDOW * first : WINDOW * last, :].rearrange("(a p) d -> p a d", p=P),
+            )
+            nc.sync.dma_start(
+                out=q_raw[:, h, first:last].rearrange("p w r d -> p w (r d)"),
+                in_=q_heads[h, WINDOW * first : WINDOW * last, :].rearrange(
+                    "(w p r) d -> p w (r d)", w=last - first, p=P, r=TILES_PER_WINDOW
                 ),
             )
+
+        for h in range(HEADS):
+            if h == 0:
+                load_keys_and_queries(h, 0, 1)
+                load_keys_and_queries(h, 1, WINDOWS)
+            else:
+                load_keys_and_queries(h, 0, WINDOWS)
+            nc.sync.dma_start(out=w_raw[:, h, :], in_=Wv[P * h : P * (h + 1), :])
             if h == 0:
                 for c in range(ROW_TILES // WORD):
                     nc.sync.dma_start(
@@ -178,35 +190,72 @@ def tile_hybridattention_pa_kernel(tc, x, Wv, q, k, out):
             return (transpose_head, keep_head)
 
         preparation = []
-        for h in range(HEADS):
+        values_position = {}
+
+        def add_keys_and_queries(h, w):
+            first_tile = TILES_PER_WINDOW * w
+            preparation.append(
+                head_entry(
+                    k_raw[:, h, first_tile : first_tile + TILES_PER_WINDOW, :],
+                    kT[:, h, WINDOW * w : WINDOW * (w + 1)],
+                )
+            )
+            preparation.append(
+                head_entry(q_raw[:, h, w], qT[:, h, w].rearrange("d r p -> d (r p)"))
+            )
+
+        def add_rows_of_wv(h):
             preparation.append(
                 rows_entry(w_raw[:, h, :], w_codes[:, h], w_scales[:, h], nc.vector.tensor_copy)
             )
-            for w in range(WINDOWS):
-                first_tile = TILES_PER_WINDOW * w
-                preparation.append(
-                    head_entry(
-                        k_raw[:, h, first_tile : first_tile + TILES_PER_WINDOW, :],
-                        kT[:, h, WINDOW * w : WINDOW * (w + 1)],
-                    )
-                )
-                preparation.append(
-                    head_entry(q_raw[:, h, w], qT[:, h, w].rearrange("d r p -> d (r p)"))
-                )
-            if h == 0:
-                for n in range(ROW_TILES):
-                    preparation.append(
-                        rows_entry(
-                            x_raw[:, n // WORD, n % WORD, :], x_codes[:, n], x_scales[:, n], nc.scalar.copy
-                        )
-                    )
-                lead = len(preparation)
-            for w in range(WINDOWS):
-                preparation.append(values_entry(w, h))
 
-        def prepare(position, lag):
-            if 0 <= position - lag < len(preparation):
-                stages = preparation[position - lag]
+        def add_rows_of_x(w):
+            for n in range(TILES_PER_WINDOW * w, TILES_PER_WINDOW * (w + 1)):
+                preparation.append(
+                    rows_entry(x_raw[:, n // WORD, n % WORD, :], x_codes[:, n], x_scales[:, n], nc.scalar.copy)
+                )
+
+        def add_values(w, h):
+            values_position[(h, w)] = len(preparation)
+            preparation.append(values_entry(w, h))
+
+        add_keys_and_queries(0, 0)
+        add_keys_and_queries(0, 1)
+        add_rows_of_wv(0)
+        add_rows_of_x(0)
+        add_keys_and_queries(0, 2)
+        add_rows_of_x(1)
+        for h in range(HEADS):
+            add_values(0, h)
+            if h < HEADS - 1:
+                add_keys_and_queries(h + 1, 0)
+            if h == 0:
+                add_rows_of_x(2)
+            if h < HEADS - 1:
+                add_keys_and_queries(h + 1, 1)
+            add_values(1, h)
+            if h < HEADS - 1:
+                add_rows_of_wv(h + 1)
+                add_keys_and_queries(h + 1, 2)
+            add_values(2, h)
+            if h == 0:
+                first_head_entries = len(preparation)
+
+        entry_step = []
+        for position in range(len(preparation)):
+            if position < LEAD:
+                entry_step.append(-LEAD)
+            elif position < first_head_entries + SPARE:
+                entry_step.append((position - LEAD) // 2)
+            else:
+                entry_step.append(entry_step[-1] + 1)
+        started_at = {}
+        for position, step in enumerate(entry_step):
+            started_at.setdefault(step, []).append(position)
+
+        def prepare(step, lag):
+            for position in started_at.get(step - lag, []):
+                stages = preparation[position]
                 if lag < len(stages):
                     stages[lag]()
 
@@ -313,8 +362,8 @@ def tile_hybridattention_pa_kernel(tc, x, Wv, q, k, out):
             regrouped_e[unit] = regrouped
 
         def quantise_e(unit):
-            codes = stage.tile([P, HALVES, P], U32, tag="e_codes", align_bytes=64)
-            scales = stage.tile([P, HALVES, P], U8, tag="e_scales", align_bytes=64)
+            codes = late.tile([P, HALVES, P], U32, tag="e_codes", align_bytes=64)
+            scales = late.tile([P, HALVES, P], U8, tag="e_scales", align_bytes=64)
             nc.vector.quantize_mx(
                 out=codes[:].rearrange("p g q -> p (g q)").bitcast(FP8X4),
                 scales=scales[:].rearrange("p g q -> p (g q)"),
@@ -371,6 +420,18 @@ def tile_hybridattention_pa_kernel(tc, x, Wv, q, k, out):
                 in_=result[:],
             )
 
+        products_at = {}
+        divide_at = {}
+        step = 0
+        for unit, (h, w, halves) in enumerate(units):
+            ready = max(entry_step[values_position[(h, kw)]] for r, kw in halves) + 2
+            step = max(step, unit + PRODUCT_LAG, ready)
+            if len(products_at.get(step, [])) == 2:
+                step = step + 1
+            products_at.setdefault(step, []).append(unit)
+            if halves[1][0] == TILES_PER_WINDOW - 1:
+                divide_at.setdefault(step + 1, []).append((h, w))
+
         def for_unit(stage_fn, unit):
             if 0 <= unit < len(units):
                 stage_fn(unit)
@@ -381,7 +442,7 @@ def tile_hybridattention_pa_kernel(tc, x, Wv, q, k, out):
                 if halves[1][0] == TILES_PER_WINDOW - 1:
                     stage_fn((h, w))
 
-        for step in range(-lead, len(units) + DIVIDE_LAG + 1):
+        for step in range(-LEAD, max(divide_at) + 1):
             for_unit(exponentiate, step - EXP_LAG)
             for_unit(compute_scores, step)
             for_unit(transpose_e, step - EXP_LAG)
@@ -391,8 +452,10 @@ def tile_hybridattention_pa_kernel(tc, x, Wv, q, k, out):
             for_group(add_row_sums, step - REGROUP_LAG)
             for_unit(quantise_e, step - QUANTISE_LAG)
             for_group(invert_row_sums, step - QUANTISE_LAG)
-            prepare(step + lead, 0)
-            for_unit(multiply_by_v, step - PRODUCT_LAG)
-            for_group(divide_and_store, step - DIVIDE_LAG)
-            prepare(step + lead, 1)
-            prepare(step + lead, 2)
+            prepare(step, 2)
+            prepare(step, 0)
+            for unit in products_at.get(step, []):
+                multiply_by_v(unit)
+            for group in divide_at.get(step, []):
+                divide_and_store(group)
+            prepare(step, 1)

@@ -53,8 +53,7 @@ def tile_hybridattention_pa_kernel(tc, x, Wv, q, k, out):
         stage = stack.enter_context(tc.tile_pool(name="stage", bufs=3))
         small = stack.enter_context(tc.tile_pool(name="small", bufs=8))
         late = stack.enter_context(tc.tile_pool(name="late", bufs=14))
-        psum_scores = stack.enter_context(tc.psum_pool(name="psum_scores", bufs=4))
-        psum_work = stack.enter_context(tc.psum_pool(name="psum_work", bufs=4))
+        psum_work = stack.enter_context(tc.psum_pool(name="psum_work", bufs=8))
 
         w_raw = keep.tile([P, HEADS, FEATURES], BF16)
         k_raw = keep.tile([P, HEADS, ROW_TILES, HEAD_DIM], BF16)
@@ -206,13 +205,23 @@ def tile_hybridattention_pa_kernel(tc, x, Wv, q, k, out):
 
         def add_rows_of_wv(h):
             preparation.append(
-                rows_entry(w_raw[:, h, :], w_codes[:, h], w_scales[:, h], nc.vector.tensor_copy)
+                rows_entry(
+                    w_raw[:, h, :],
+                    w_codes[:, h],
+                    w_scales[:, h],
+                    nc.scalar.copy if h == 0 else nc.vector.tensor_copy,
+                )
             )
 
         def add_rows_of_x(w):
             for n in range(TILES_PER_WINDOW * w, TILES_PER_WINDOW * (w + 1)):
                 preparation.append(
-                    rows_entry(x_raw[:, n // WORD, n % WORD, :], x_codes[:, n], x_scales[:, n], nc.scalar.copy)
+                    rows_entry(
+                        x_raw[:, n // WORD, n % WORD, :],
+                        x_codes[:, n],
+                        x_scales[:, n],
+                        nc.scalar.copy if n % 2 == 0 else nc.vector.tensor_copy,
+                    )
                 )
 
         def add_values(w, h):
@@ -282,11 +291,21 @@ def tile_hybridattention_pa_kernel(tc, x, Wv, q, k, out):
         inverses = {}
         products = {}
 
+        def portions(unit):
+            if unit == len(units) - 1:
+                return [(0, 1), (1, HALVES)]
+            return [(0, HALVES)]
+
+        def query_portions(group):
+            if group == (HEADS - 1, WINDOWS - 1):
+                return [(0, TILES_PER_WINDOW - 1), (TILES_PER_WINDOW - 1, TILES_PER_WINDOW)]
+            return [(0, TILES_PER_WINDOW)]
+
         def compute_scores(unit):
             h, w, halves = units[unit]
             score_banks[unit] = []
             for r, kw in halves:
-                bank = psum_scores.tile([P, WINDOW], F32, tag="scores")
+                bank = psum_work.tile([P, WINDOW], F32, tag="work")
                 nc.tensor.matmul(
                     out=bank[:],
                     lhsT=qT[:, h, w, r, :],
@@ -309,9 +328,15 @@ def tile_hybridattention_pa_kernel(tc, x, Wv, q, k, out):
             maxima = row_maxima[unit]
             bias = small.tile([P, HALVES], F32, tag="bias")
             if w == 0:
-                nc.gpsimd.tensor_scalar(
-                    out=bias[:], in0=maxima[:], scalar1=-SCALE, scalar2=0.0, op0=ALU.mult, op1=ALU.add
-                )
+                for g in range(HALVES):
+                    nc.gpsimd.tensor_scalar(
+                        out=bias[:, g : g + 1],
+                        in0=maxima[:, g : g + 1],
+                        scalar1=-SCALE,
+                        scalar2=0.0,
+                        op0=ALU.mult,
+                        op1=ALU.add,
+                    )
             else:
                 nc.gpsimd.tensor_scalar(
                     out=bias[:, 0:1],
@@ -345,41 +370,49 @@ def tile_hybridattention_pa_kernel(tc, x, Wv, q, k, out):
 
         def transpose_e(unit):
             words = exponentials[unit][:].bitcast(F32)
-            transposed = psum_work.tile([P, HALVES, PAIRS, P], F32, tag="work")
-            for g in range(HALVES):
-                for u in range(PAIRS):
-                    slab = PAIRS * g + u
-                    nc.tensor.transpose(
-                        transposed[:, g, u, :], words[:, slab * P : (slab + 1) * P], ident_f32[:]
-                    )
-            transposed_e[unit] = transposed
+            transposed_e[unit] = []
+            for first, last in portions(unit):
+                transposed = psum_work.tile([P, HALVES, PAIRS, P], F32, tag="work")
+                for g in range(first, last):
+                    for u in range(PAIRS):
+                        slab = PAIRS * g + u
+                        nc.tensor.transpose(
+                            transposed[:, g, u, :], words[:, slab * P : (slab + 1) * P], ident_f32[:]
+                        )
+                transposed_e[unit].append(transposed)
 
         def regroup_e(unit):
             regrouped = stage.tile([P, HALVES, P, PAIRS], F32, tag="regrouped_e", align_bytes=64)
-            nc.scalar.copy(
-                out=regrouped[:], in_=transposed_e[unit][:].rearrange("p g u q -> p g q u")
-            )
+            copy_out = nc.vector.tensor_copy if unit >= len(units) - 3 else nc.scalar.copy
+            for transposed, (first, last) in zip(transposed_e[unit], portions(unit)):
+                copy_out(
+                    out=regrouped[:, first:last],
+                    in_=transposed[:, first:last].rearrange("p g u q -> p g q u"),
+                )
             regrouped_e[unit] = regrouped
 
         def quantise_e(unit):
             codes = late.tile([P, HALVES, P], U32, tag="e_codes", align_bytes=64)
             scales = late.tile([P, HALVES, P], U8, tag="e_scales", align_bytes=64)
-            nc.vector.quantize_mx(
-                out=codes[:].rearrange("p g q -> p (g q)").bitcast(FP8X4),
-                scales=scales[:].rearrange("p g q -> p (g q)"),
-                in_=regrouped_e[unit][:].rearrange("p g q u -> p (g q u)").bitcast(BF16),
-            )
+            for first, last in portions(unit):
+                nc.vector.quantize_mx(
+                    out=codes[:, first:last].rearrange("p g q -> p (g q)").bitcast(FP8X4),
+                    scales=scales[:, first:last].rearrange("p g q -> p (g q)"),
+                    in_=regrouped_e[unit][:, first:last].rearrange("p g q u -> p (g q u)").bitcast(BF16),
+                )
             e_codes[unit] = codes
             e_scales[unit] = scales
 
         def multiply_by_v(unit):
             h, w, halves = units[unit]
-            if halves[0][0] == 0:
-                product = psum_work.tile([P, TILES_PER_WINDOW, HEAD_DIM], F32, tag="work")
-                products[(h, w)] = product
+            for first, last in query_portions((h, w)):
+                if halves[0][0] == first:
+                    product = psum_work.tile([P, TILES_PER_WINDOW, HEAD_DIM], F32, tag="work")
+                    for r in range(first, last):
+                        products[(h, w, r)] = product
             for g, (r, kw) in enumerate(halves):
                 nc.tensor.matmul_mx(
-                    out=products[(h, w)][:, r, :],
+                    out=products[(h, w, r)][:, r, :],
                     lhsT=e_codes[unit][:, g, :].bitcast(FP8X4),
                     lhsT_scale=e_scales[unit][:, g, :],
                     rhs=v_codes[:, kw, h, :].bitcast(FP8X4),
@@ -394,43 +427,52 @@ def tile_hybridattention_pa_kernel(tc, x, Wv, q, k, out):
                 denominators[group] = sums[:, :, 0]
             else:
                 total = small.tile([P, TILES_PER_WINDOW], F32, tag="total")
-                nc.gpsimd.tensor_tensor(
-                    out=total[:], in0=sums[:, :, 0], in1=sums[:, :, 1], op=ALU.add
-                )
+                for first, last in query_portions(group):
+                    nc.gpsimd.tensor_tensor(
+                        out=total[:, first:last],
+                        in0=sums[:, first:last, 0],
+                        in1=sums[:, first:last, 1],
+                        op=ALU.add,
+                    )
                 denominators[group] = total[:]
 
         def invert_row_sums(group):
             inverse = small.tile([P, TILES_PER_WINDOW], F32, tag="inverse")
-            nc.vector.reciprocal(out=inverse[:], in_=denominators[group])
+            for first, last in query_portions(group):
+                nc.vector.reciprocal(
+                    out=inverse[:, first:last], in_=denominators[group][:, first:last]
+                )
             inverses[group] = inverse
 
         def divide_and_store(group):
             h, w = group
             result = stage.tile([P, TILES_PER_WINDOW, HEAD_DIM], F32, tag="result")
-            nc.vector.tensor_tensor(
-                out=result[:],
-                in0=products[group][:],
-                in1=inverses[group][:].unsqueeze(2).to_broadcast([P, TILES_PER_WINDOW, HEAD_DIM]),
-                op=ALU.mult,
-            )
-            nc.sync.dma_start(
-                out=out_rows[
-                    WINDOW * w : WINDOW * (w + 1), HEAD_DIM * h : HEAD_DIM * (h + 1)
-                ].rearrange("(p r) d -> p r d", r=TILES_PER_WINDOW),
-                in_=result[:],
-            )
+            rows_out = out_rows[
+                WINDOW * w : WINDOW * (w + 1), HEAD_DIM * h : HEAD_DIM * (h + 1)
+            ].rearrange("(p r) d -> p r d", r=TILES_PER_WINDOW)
+            for first, last in query_portions(group):
+                nc.vector.tensor_tensor(
+                    out=result[:, first:last],
+                    in0=products[(h, w, first)][:, first:last],
+                    in1=inverses[group][:, first:last]
+                    .unsqueeze(2)
+                    .to_broadcast([P, last - first, HEAD_DIM]),
+                    op=ALU.mult,
+                )
+                nc.sync.dma_start(out=rows_out[:, first:last], in_=result[:, first:last])
 
         products_at = {}
         divide_at = {}
         step = 0
+        group_units = []
         for unit, (h, w, halves) in enumerate(units):
-            ready = max(entry_step[values_position[(h, kw)]] for r, kw in halves) + 2
-            step = max(step, unit + PRODUCT_LAG, ready)
-            if len(products_at.get(step, [])) == 2:
-                step = step + 1
-            products_at.setdefault(step, []).append(unit)
+            group_units.append(unit)
             if halves[1][0] == TILES_PER_WINDOW - 1:
-                divide_at.setdefault(step + 1, []).append((h, w))
+                ready = max(entry_step[values_position[(h, kw)]] for r, kw in halves) + 2
+                step = max(step + 1, unit + PRODUCT_LAG, ready)
+                products_at[step] = group_units
+                divide_at[step + 1] = [(h, w)]
+                group_units = []
 
         def for_unit(stage_fn, unit):
             if 0 <= unit < len(units):

@@ -50,7 +50,7 @@ def tile_hybridattention_pa_kernel(tc, x, Wv, q, k, out):
 
     with ExitStack() as stack:
         keep = stack.enter_context(tc.tile_pool(name="keep", bufs=1))
-        stage = stack.enter_context(tc.tile_pool(name="stage", bufs=3))
+        stage = stack.enter_context(tc.tile_pool(name="stage", bufs=4))
         small = stack.enter_context(tc.tile_pool(name="small", bufs=8))
         late = stack.enter_context(tc.tile_pool(name="late", bufs=14))
         psum_work = stack.enter_context(tc.psum_pool(name="psum_work", bufs=8))
@@ -220,7 +220,7 @@ def tile_hybridattention_pa_kernel(tc, x, Wv, q, k, out):
                         x_raw[:, n // WORD, n % WORD, :],
                         x_codes[:, n],
                         x_scales[:, n],
-                        nc.scalar.copy if n % 2 == 0 else nc.vector.tensor_copy,
+                        nc.vector.tensor_copy if n % 4 == 3 else nc.scalar.copy,
                     )
                 )
 
@@ -484,20 +484,21 @@ def tile_hybridattention_pa_kernel(tc, x, Wv, q, k, out):
                 if halves[1][0] == TILES_PER_WINDOW - 1:
                     stage_fn((h, w))
 
+        stack.enter_context(tc.manual_schedule())
         for step in range(-LEAD, max(divide_at) + 1):
-            for_unit(exponentiate, step - EXP_LAG)
-            for_unit(compute_scores, step)
-            for_unit(transpose_e, step - EXP_LAG)
-            for_unit(regroup_e, step - REGROUP_LAG)
             for_unit(find_maxima, step - MAXIMA_LAG)
             for_unit(make_bias, step - MAXIMA_LAG)
+            prepare(step, 1)
+            for_unit(exponentiate, step - EXP_LAG)
             for_group(add_row_sums, step - REGROUP_LAG)
-            for_unit(quantise_e, step - QUANTISE_LAG)
-            for_group(invert_row_sums, step - QUANTISE_LAG)
             prepare(step, 2)
+            for_group(invert_row_sums, step - QUANTISE_LAG)
+            for_unit(quantise_e, step - QUANTISE_LAG)
+            for group in divide_at.get(step, []):
+                divide_and_store(group)
+            for_unit(regroup_e, step - REGROUP_LAG)
+            for_unit(compute_scores, step)
             prepare(step, 0)
             for unit in products_at.get(step, []):
                 multiply_by_v(unit)
-            for group in divide_at.get(step, []):
-                divide_and_store(group)
-            prepare(step, 1)
+            for_unit(transpose_e, step - EXP_LAG)

@@ -36,7 +36,9 @@ REGROUP_LAG = 3
 QUANTISE_LAG = 4
 PRODUCT_LAG = 5
 LEAD = 2
-SPARE = 6
+FIRST_STEP = -2
+SPARE = 4
+LAST_GROUP = (HEADS - 1, WINDOWS - 1)
 
 FLOPS = 2 * SEQ * FEATURES * FEATURES + 2 * (2 * HEADS * SEQ * 2 * WINDOW * HEAD_DIM)
 
@@ -103,7 +105,7 @@ def tile_hybridattention_pa_kernel(tc, x, Wv, q, k, out):
         x_codes = keep.tile([P, ROW_TILES, FEATURE_PASSES, P], U32, align_bytes=64)
         x_scales = keep.tile([P, ROW_TILES, FEATURE_PASSES, P], U8, align_bytes=64)
 
-        def rows_entry(rows, codes, scales, copy_out):
+        def rows_entry(rows, codes, scales, by_vector):
             tiles = {}
 
             def transpose_rows():
@@ -117,6 +119,7 @@ def tile_hybridattention_pa_kernel(tc, x, Wv, q, k, out):
 
             def regroup_rows():
                 regrouped = stage.tile([P, FEATURE_PASSES, P, PAIRS], F32, tag="rows", align_bytes=64)
+                copy_out = nc.vector.tensor_copy if by_vector else nc.scalar.copy
                 copy_out(
                     out=regrouped[:],
                     in_=tiles["transposed"][:].rearrange("p (c u) t -> p c t u", u=PAIRS),
@@ -130,7 +133,8 @@ def tile_hybridattention_pa_kernel(tc, x, Wv, q, k, out):
                     in_=tiles["regrouped"][:].rearrange("p c t u -> p (c t u)").bitcast(BF16),
                 )
 
-            return (transpose_rows, regroup_rows, quantise_rows)
+            copy_stage = "vector copy" if by_vector else "scalar copy"
+            return {"matmuls": transpose_rows, copy_stage: regroup_rows, "quantise": quantise_rows}
 
         v_codes = keep.tile([P, WINDOWS, HEADS, HEAD_DIM], U32, align_bytes=64)
         v_scales = keep.tile([P, WINDOWS, HEADS, HEAD_DIM], U8, align_bytes=64)
@@ -167,7 +171,7 @@ def tile_hybridattention_pa_kernel(tc, x, Wv, q, k, out):
                     in_=tiles["regrouped"][:].rearrange("p d j -> p (d j)"),
                 )
 
-            return (project, regroup_values, quantise_values)
+            return {"matmuls": project, "scalar copy": regroup_values, "quantise": quantise_values}
 
         kT = keep.tile([P, HEADS, SEQ], BF16)
         qT = keep.tile([P, HEADS, WINDOWS, TILES_PER_WINDOW, P], BF16)
@@ -186,7 +190,7 @@ def tile_hybridattention_pa_kernel(tc, x, Wv, q, k, out):
                     out=place, in_=tiles["transposed"][:].rearrange("d a p -> d (a p)")
                 )
 
-            return (transpose_head, keep_head)
+            return {"matmuls": transpose_head, "vector copy": keep_head}
 
         preparation = []
         values_position = {}
@@ -209,7 +213,7 @@ def tile_hybridattention_pa_kernel(tc, x, Wv, q, k, out):
                     w_raw[:, h, :],
                     w_codes[:, h],
                     w_scales[:, h],
-                    nc.scalar.copy if h == 0 else nc.vector.tensor_copy,
+                    by_vector=h > 0,
                 )
             )
 
@@ -220,7 +224,7 @@ def tile_hybridattention_pa_kernel(tc, x, Wv, q, k, out):
                         x_raw[:, n // WORD, n % WORD, :],
                         x_codes[:, n],
                         x_scales[:, n],
-                        nc.vector.tensor_copy if n % 4 == 3 else nc.scalar.copy,
+                        by_vector=n % 4 == 3,
                     )
                 )
 
@@ -262,11 +266,10 @@ def tile_hybridattention_pa_kernel(tc, x, Wv, q, k, out):
         for position, step in enumerate(entry_step):
             started_at.setdefault(step, []).append(position)
 
-        def prepare(step, lag):
-            for position in started_at.get(step - lag, []):
-                stages = preparation[position]
-                if lag < len(stages):
-                    stages[lag]()
+        def prepare(stage_name, start):
+            for position in started_at.get(start, []):
+                if stage_name in preparation[position]:
+                    preparation[position][stage_name]()
 
         units = []
         for h in range(HEADS):
@@ -290,6 +293,7 @@ def tile_hybridattention_pa_kernel(tc, x, Wv, q, k, out):
         denominators = {}
         inverses = {}
         products = {}
+        results = {}
 
         def portions(unit):
             if unit == len(units) - 1:
@@ -297,7 +301,7 @@ def tile_hybridattention_pa_kernel(tc, x, Wv, q, k, out):
             return [(0, HALVES)]
 
         def query_portions(group):
-            if group == (HEADS - 1, WINDOWS - 1):
+            if group == LAST_GROUP:
                 return [(0, TILES_PER_WINDOW - 1), (TILES_PER_WINDOW - 1, TILES_PER_WINDOW)]
             return [(0, TILES_PER_WINDOW)]
 
@@ -368,49 +372,48 @@ def tile_hybridattention_pa_kernel(tc, x, Wv, q, k, out):
                 )
             exponentials[unit] = e
 
-        def transpose_e(unit):
+        def transpose_e(unit, first, last):
             words = exponentials[unit][:].bitcast(F32)
-            transposed_e[unit] = []
-            for first, last in portions(unit):
-                transposed = psum_work.tile([P, HALVES, PAIRS, P], F32, tag="work")
-                for g in range(first, last):
-                    for u in range(PAIRS):
-                        slab = PAIRS * g + u
-                        nc.tensor.transpose(
-                            transposed[:, g, u, :], words[:, slab * P : (slab + 1) * P], ident_f32[:]
-                        )
-                transposed_e[unit].append(transposed)
+            transposed = psum_work.tile([P, HALVES, PAIRS, P], F32, tag="work")
+            for g in range(first, last):
+                for u in range(PAIRS):
+                    slab = PAIRS * g + u
+                    nc.tensor.transpose(
+                        transposed[:, g, u, :], words[:, slab * P : (slab + 1) * P], ident_f32[:]
+                    )
+            transposed_e[(unit, first)] = transposed
 
-        def regroup_e(unit):
-            regrouped = stage.tile([P, HALVES, P, PAIRS], F32, tag="regrouped_e", align_bytes=64)
-            copy_out = nc.vector.tensor_copy if unit >= len(units) - 3 else nc.scalar.copy
-            for transposed, (first, last) in zip(transposed_e[unit], portions(unit)):
-                copy_out(
-                    out=regrouped[:, first:last],
-                    in_=transposed[:, first:last].rearrange("p g u q -> p g q u"),
-                )
-            regrouped_e[unit] = regrouped
+        def regroup_e(unit, first, last):
+            if first == 0:
+                regrouped = stage.tile([P, HALVES, P, PAIRS], F32, tag="regrouped_e", align_bytes=64)
+                regrouped_e[unit] = regrouped
+            copy_out = nc.vector.tensor_copy if unit >= len(units) - 3 and first == 0 else nc.scalar.copy
+            copy_out(
+                out=regrouped_e[unit][:, first:last],
+                in_=transposed_e[(unit, first)][:, first:last].rearrange("p g u q -> p g q u"),
+            )
 
-        def quantise_e(unit):
-            codes = late.tile([P, HALVES, P], U32, tag="e_codes", align_bytes=64)
-            scales = late.tile([P, HALVES, P], U8, tag="e_scales", align_bytes=64)
-            for first, last in portions(unit):
-                nc.vector.quantize_mx(
-                    out=codes[:, first:last].rearrange("p g q -> p (g q)").bitcast(FP8X4),
-                    scales=scales[:, first:last].rearrange("p g q -> p (g q)"),
-                    in_=regrouped_e[unit][:, first:last].rearrange("p g q u -> p (g q u)").bitcast(BF16),
-                )
-            e_codes[unit] = codes
-            e_scales[unit] = scales
+        def quantise_e(unit, first, last):
+            if first == 0:
+                codes = late.tile([P, HALVES, P], U32, tag="e_codes", align_bytes=64)
+                scales = late.tile([P, HALVES, P], U8, tag="e_scales", align_bytes=64)
+                e_codes[unit] = codes
+                e_scales[unit] = scales
+            nc.vector.quantize_mx(
+                out=e_codes[unit][:, first:last].rearrange("p g q -> p (g q)").bitcast(FP8X4),
+                scales=e_scales[unit][:, first:last].rearrange("p g q -> p (g q)"),
+                in_=regrouped_e[unit][:, first:last].rearrange("p g q u -> p (g q u)").bitcast(BF16),
+            )
 
-        def multiply_by_v(unit):
+        def multiply_by_v(unit, first, last):
             h, w, halves = units[unit]
-            for first, last in query_portions((h, w)):
-                if halves[0][0] == first:
+            for first_tile, last_tile in query_portions((h, w)):
+                if halves[0][0] == first_tile and first == 0:
                     product = psum_work.tile([P, TILES_PER_WINDOW, HEAD_DIM], F32, tag="work")
-                    for r in range(first, last):
+                    for r in range(first_tile, last_tile):
                         products[(h, w, r)] = product
-            for g, (r, kw) in enumerate(halves):
+            for g in range(first, last):
+                r, kw = halves[g]
                 nc.tensor.matmul_mx(
                     out=products[(h, w, r)][:, r, :],
                     lhsT=e_codes[unit][:, g, :].bitcast(FP8X4),
@@ -421,84 +424,98 @@ def tile_hybridattention_pa_kernel(tc, x, Wv, q, k, out):
                     stop=(w == 0 or g == HALVES - 1),
                 )
 
-        def add_row_sums(group):
+        def add_row_sums(group, first, last):
             sums = row_sums[group]
             if group[1] == 0:
                 denominators[group] = sums[:, :, 0]
             else:
-                total = small.tile([P, TILES_PER_WINDOW], F32, tag="total")
-                for first, last in query_portions(group):
-                    nc.gpsimd.tensor_tensor(
-                        out=total[:, first:last],
-                        in0=sums[:, first:last, 0],
-                        in1=sums[:, first:last, 1],
-                        op=ALU.add,
-                    )
-                denominators[group] = total[:]
-
-        def invert_row_sums(group):
-            inverse = small.tile([P, TILES_PER_WINDOW], F32, tag="inverse")
-            for first, last in query_portions(group):
-                nc.vector.reciprocal(
-                    out=inverse[:, first:last], in_=denominators[group][:, first:last]
+                if first == 0:
+                    total = small.tile([P, TILES_PER_WINDOW], F32, tag="total")
+                    denominators[group] = total[:]
+                nc.gpsimd.tensor_tensor(
+                    out=denominators[group][:, first:last],
+                    in0=sums[:, first:last, 0],
+                    in1=sums[:, first:last, 1],
+                    op=ALU.add,
                 )
-            inverses[group] = inverse
 
-        def divide_and_store(group):
+        def invert_row_sums(group, first, last):
+            if first == 0:
+                inverse = small.tile([P, TILES_PER_WINDOW], F32, tag="inverse")
+                inverses[group] = inverse
+            nc.vector.reciprocal(
+                out=inverses[group][:, first:last], in_=denominators[group][:, first:last]
+            )
+
+        def divide_and_store(group, first, last):
             h, w = group
-            result = stage.tile([P, TILES_PER_WINDOW, HEAD_DIM], F32, tag="result")
-            rows_out = out_rows[
-                WINDOW * w : WINDOW * (w + 1), HEAD_DIM * h : HEAD_DIM * (h + 1)
-            ].rearrange("(p r) d -> p r d", r=TILES_PER_WINDOW)
-            for first, last in query_portions(group):
-                nc.vector.tensor_tensor(
-                    out=result[:, first:last],
-                    in0=products[(h, w, first)][:, first:last],
-                    in1=inverses[group][:, first:last]
-                    .unsqueeze(2)
-                    .to_broadcast([P, last - first, HEAD_DIM]),
-                    op=ALU.mult,
-                )
-                nc.sync.dma_start(out=rows_out[:, first:last], in_=result[:, first:last])
+            if first == 0:
+                result = stage.tile([P, TILES_PER_WINDOW, HEAD_DIM], F32, tag="result")
+                results[group] = result
+            nc.vector.tensor_tensor(
+                out=results[group][:, first:last],
+                in0=products[(h, w, first)][:, first:last],
+                in1=inverses[group][:, first:last].unsqueeze(2).to_broadcast([P, last - first, HEAD_DIM]),
+                op=ALU.mult,
+            )
+            nc.sync.dma_start(
+                out=out_rows[
+                    WINDOW * w : WINDOW * (w + 1), HEAD_DIM * h : HEAD_DIM * (h + 1)
+                ].rearrange("(p r) d -> p r d", r=TILES_PER_WINDOW)[:, first:last],
+                in_=results[group][:, first:last],
+            )
 
         products_at = {}
         divide_at = {}
         step = 0
         group_units = []
         for unit, (h, w, halves) in enumerate(units):
-            group_units.append(unit)
-            if halves[1][0] == TILES_PER_WINDOW - 1:
-                ready = max(entry_step[values_position[(h, kw)]] for r, kw in halves) + 2
+            group_units.append((unit, 0, HALVES))
+            ready = max(entry_step[values_position[(h, kw)]] for r, kw in halves) + 2
+            if (h, w) == LAST_GROUP:
+                for number, (first, last) in enumerate(portions(unit)):
+                    step = unit + PRODUCT_LAG + number
+                    products_at[step] = [(unit, first, last)]
+            elif halves[1][0] == TILES_PER_WINDOW - 1:
                 step = max(step + 1, unit + PRODUCT_LAG, ready)
                 products_at[step] = group_units
-                divide_at[step + 1] = [(h, w)]
                 group_units = []
+            for first, last in query_portions((h, w)):
+                if halves[1][0] == last - 1:
+                    divide_at.setdefault(step + 1, []).append(((h, w), first, last))
 
         def for_unit(stage_fn, unit):
             if 0 <= unit < len(units):
                 stage_fn(unit)
 
-        def for_group(stage_fn, unit):
+        def for_portions(stage_fn, unit):
+            for number in range(HALVES):
+                if 0 <= unit - number < len(units) and number < len(portions(unit - number)):
+                    stage_fn(unit - number, *portions(unit - number)[number])
+
+        def for_query_portions(stage_fn, unit):
             if 0 <= unit < len(units):
                 h, w, halves = units[unit]
-                if halves[1][0] == TILES_PER_WINDOW - 1:
-                    stage_fn((h, w))
+                for first, last in query_portions((h, w)):
+                    if halves[1][0] == last - 1:
+                        stage_fn((h, w), first, last)
 
         stack.enter_context(tc.manual_schedule())
-        for step in range(-LEAD, max(divide_at) + 1):
+        for step in range(FIRST_STEP, max(divide_at) + 1):
             for_unit(find_maxima, step - MAXIMA_LAG)
             for_unit(make_bias, step - MAXIMA_LAG)
-            prepare(step, 1)
+            prepare("vector copy", step - 1)
             for_unit(exponentiate, step - EXP_LAG)
-            for_group(add_row_sums, step - REGROUP_LAG)
-            prepare(step, 2)
-            for_group(invert_row_sums, step - QUANTISE_LAG)
-            for_unit(quantise_e, step - QUANTISE_LAG)
-            for group in divide_at.get(step, []):
-                divide_and_store(group)
-            for_unit(regroup_e, step - REGROUP_LAG)
+            prepare("scalar copy", step - 1)
+            for_query_portions(add_row_sums, step - REGROUP_LAG)
+            prepare("quantise", step - 2)
+            for_query_portions(invert_row_sums, step - QUANTISE_LAG)
+            for group, first, last in divide_at.get(step, []):
+                divide_and_store(group, first, last)
+            for_portions(quantise_e, step - QUANTISE_LAG)
+            for_portions(regroup_e, step - REGROUP_LAG)
             for_unit(compute_scores, step)
-            prepare(step, 0)
-            for unit in products_at.get(step, []):
-                multiply_by_v(unit)
-            for_unit(transpose_e, step - EXP_LAG)
+            prepare("matmuls", step)
+            for unit, first, last in products_at.get(step, []):
+                multiply_by_v(unit, first, last)
+            for_portions(transpose_e, step - EXP_LAG)

@@ -61,12 +61,12 @@ def tile_hybridattention_pa_kernel(tc, x, Wv, q, k, out):
         k_raw = keep.tile([P, HEADS, ROW_TILES, HEAD_DIM], BF16)
         q_raw = keep.tile([P, HEADS, WINDOWS, TILES_PER_WINDOW, HEAD_DIM], BF16)
         x_raw = keep.tile([P, ROW_TILES // WORD, WORD, FEATURES], BF16)
-        def load_keys_and_queries(h, first, last):
+        def load_keys_and_queries(h, first, last, q_queue=nc.sync):
             nc.sync.dma_start(
                 out=k_raw[:, h, TILES_PER_WINDOW * first : TILES_PER_WINDOW * last, :],
                 in_=k_heads[h, WINDOW * first : WINDOW * last, :].rearrange("(a p) d -> p a d", p=P),
             )
-            nc.sync.dma_start(
+            q_queue.dma_start(
                 out=q_raw[:, h, first:last].rearrange("p w r d -> p w (r d)"),
                 in_=q_heads[h, WINDOW * first : WINDOW * last, :].rearrange(
                     "(w p r) d -> p w (r d)", w=last - first, p=P, r=TILES_PER_WINDOW
@@ -75,7 +75,7 @@ def tile_hybridattention_pa_kernel(tc, x, Wv, q, k, out):
 
         for h in range(HEADS):
             if h == 0:
-                load_keys_and_queries(h, 0, 1)
+                load_keys_and_queries(h, 0, 1, q_queue=nc.scalar)
                 load_keys_and_queries(h, 1, WINDOWS)
             else:
                 load_keys_and_queries(h, 0, WINDOWS)
@@ -89,10 +89,10 @@ def tile_hybridattention_pa_kernel(tc, x, Wv, q, k, out):
                         ),
                     )
 
-        ident_f32 = keep.tile([P, P], F32)
-        make_identity(nc, ident_f32[:])
         ident_bf16 = keep.tile([P, P], BF16)
         make_identity(nc, ident_bf16[:])
+        ident_f32 = keep.tile([P, P], F32)
+        make_identity(nc, ident_f32[:])
 
         zero = keep.tile([P, 1], F32)
         nc.vector.memset(zero[:], 0.0)

@@ -387,7 +387,8 @@ def tile_hybridattention_pa_kernel(tc, x, Wv, q, k, out):
             if first == 0:
                 regrouped = stage.tile([P, HALVES, P, PAIRS], F32, tag="regrouped_e", align_bytes=64)
                 regrouped_e[unit] = regrouped
-            copy_out = nc.vector.tensor_copy if unit >= len(units) - 3 and first == 0 else nc.scalar.copy
+            by_vector = len(units) - 3 <= unit < len(units) - 1
+            copy_out = nc.vector.tensor_copy if by_vector else nc.scalar.copy
             copy_out(
                 out=regrouped_e[unit][:, first:last],
                 in_=transposed_e[(unit, first)][:, first:last].rearrange("p g u q -> p g q u"),
@@ -510,9 +511,9 @@ def tile_hybridattention_pa_kernel(tc, x, Wv, q, k, out):
             for_query_portions(add_row_sums, step - REGROUP_LAG)
             prepare("quantise", step - 2)
             for_query_portions(invert_row_sums, step - QUANTISE_LAG)
+            for_portions(quantise_e, step - QUANTISE_LAG)
             for group, first, last in divide_at.get(step, []):
                 divide_and_store(group, first, last)
-            for_portions(quantise_e, step - QUANTISE_LAG)
             for_portions(regroup_e, step - REGROUP_LAG)
             for_unit(compute_scores, step)
             prepare("matmuls", step)

@@ -54,7 +54,8 @@ def tile_hybridattention_pa_kernel(tc, x, Wv, q, k, out):
         keep = stack.enter_context(tc.tile_pool(name="keep", bufs=1))
         stage = stack.enter_context(tc.tile_pool(name="stage", bufs=4))
         small = stack.enter_context(tc.tile_pool(name="small", bufs=8))
-        late = stack.enter_context(tc.tile_pool(name="late", bufs=14))
+        late = stack.enter_context(tc.tile_pool(name="late", bufs=7))
+        pairs = stack.enter_context(tc.tile_pool(name="pairs", bufs=3))
         psum_work = stack.enter_context(tc.psum_pool(name="psum_work", bufs=8))
 
         w_raw = keep.tile([P, HEADS, FEATURES], BF16)
@@ -384,27 +385,41 @@ def tile_hybridattention_pa_kernel(tc, x, Wv, q, k, out):
             transposed_e[(unit, first)] = transposed
 
         def regroup_e(unit, first, last):
-            if first == 0:
-                regrouped = stage.tile([P, HALVES, P, PAIRS], F32, tag="regrouped_e", align_bytes=64)
-                regrouped_e[unit] = regrouped
+            if unit % 2 == 0:
+                pair = pairs.tile([P, 2, HALVES, P, PAIRS], F32, tag="regrouped_e", align_bytes=64)
+                regrouped_e[unit // 2] = pair
+            regrouped = regrouped_e[unit // 2][:, unit % 2]
             by_vector = len(units) - 3 <= unit < len(units) - 1
             copy_out = nc.vector.tensor_copy if by_vector else nc.scalar.copy
             copy_out(
-                out=regrouped_e[unit][:, first:last],
+                out=regrouped[:, first:last],
                 in_=transposed_e[(unit, first)][:, first:last].rearrange("p g u q -> p g q u"),
             )
 
         def quantise_e(unit, first, last):
-            if first == 0:
-                codes = late.tile([P, HALVES, P], U32, tag="e_codes", align_bytes=64)
-                scales = late.tile([P, HALVES, P], U8, tag="e_scales", align_bytes=64)
-                e_codes[unit] = codes
-                e_scales[unit] = scales
-            nc.vector.quantize_mx(
-                out=e_codes[unit][:, first:last].rearrange("p g q -> p (g q)").bitcast(FP8X4),
-                scales=e_scales[unit][:, first:last].rearrange("p g q -> p (g q)"),
-                in_=regrouped_e[unit][:, first:last].rearrange("p g q u -> p (g q u)").bitcast(BF16),
-            )
+            last_pair = unit >= len(units) - 2
+            if unit % 2 == 0:
+                codes = late.tile([P, 2, HALVES, P], U32, tag="e_codes", align_bytes=64)
+                scales = late.tile([P, 2, HALVES, P], U8, tag="e_scales", align_bytes=64)
+                for n in range(2):
+                    e_codes[unit + n] = codes[:, n]
+                    e_scales[unit + n] = scales[:, n]
+                e_codes[(unit // 2, "pair")] = codes
+                e_scales[(unit // 2, "pair")] = scales
+            if last_pair:
+                nc.vector.quantize_mx(
+                    out=e_codes[unit][:, first:last].rearrange("p g q -> p (g q)").bitcast(FP8X4),
+                    scales=e_scales[unit][:, first:last].rearrange("p g q -> p (g q)"),
+                    in_=regrouped_e[unit // 2][:, unit % 2, first:last]
+                    .rearrange("p g q u -> p (g q u)")
+                    .bitcast(BF16),
+                )
+            elif unit % 2 == 1:
+                nc.vector.quantize_mx(
+                    out=e_codes[(unit // 2, "pair")][:].rearrange("p n g q -> p (n g q)").bitcast(FP8X4),
+                    scales=e_scales[(unit // 2, "pair")][:].rearrange("p n g q -> p (n g q)"),
+                    in_=regrouped_e[unit // 2][:].rearrange("p n g q u -> p (n g q u)").bitcast(BF16),
+                )
 
         def multiply_by_v(unit, first, last):
             h, w, halves = units[unit]

@@ -38,6 +38,7 @@ PRODUCT_LAG = 5
 LEAD = 2
 FIRST_STEP = -2
 SPARE = 4
+UNITS_PER_HEAD = 10
 LAST_GROUP = (HEADS - 1, WINDOWS - 1)
 
 FLOPS = 2 * SEQ * FEATURES * FEATURES + 2 * (2 * HEADS * SEQ * 2 * WINDOW * HEAD_DIM)
@@ -389,7 +390,7 @@ def tile_hybridattention_pa_kernel(tc, x, Wv, q, k, out):
                 pair = pairs.tile([P, 2, HALVES, P, PAIRS], F32, tag="regrouped_e", align_bytes=64)
                 regrouped_e[unit // 2] = pair
             regrouped = regrouped_e[unit // 2][:, unit % 2]
-            by_vector = len(units) - 3 <= unit < len(units) - 1
+            by_vector = len(units) - 3 <= unit < len(units) - 1 or unit == len(units) - UNITS_PER_HEAD + 1
             copy_out = nc.vector.tensor_copy if by_vector else nc.scalar.copy
             copy_out(
                 out=regrouped[:, first:last],

from contextlib import ExitStack

import concourse.mybir as mybir
from concourse.masks import make_identity

BF16 = mybir.dt.bfloat16
F32 = mybir.dt.float32
U32 = mybir.dt.uint32
U8 = mybir.dt.uint8
FP8X4 = mybir.dt.float8_e4m3fn_x4
EXP = mybir.ActivationFunctionType.Exp
ALU = mybir.AluOpType
AXIS_X = mybir.AxisListType.X

P = 128
PACK = 4
WORD = 2
PAIRS = PACK // WORD
K_PASS = P * PACK
HEADS = 8
HEAD_DIM = 128
SEQ = 1536
FEATURES = 1024
WINDOW = 512
WINDOWS = SEQ // WINDOW
ROW_TILES = SEQ // P
TILES_PER_WINDOW = WINDOW // P
FEATURE_PASSES = FEATURES // K_PASS
WORD_SLABS = FEATURES // (WORD * P)
HALVES = 2
SCALE = HEAD_DIM**-0.5

MAXIMA_LAG = 1
EXP_LAG = 2
REGROUP_LAG = 3
QUANTISE_LAG = 4
PRODUCT_LAG = 5
LEAD = 2
FIRST_STEP = -2
SPARE = 4
UNITS_PER_HEAD = 10
LAST_GROUP = (HEADS - 1, WINDOWS - 1)

FLOPS = 2 * SEQ * FEATURES * FEATURES + 2 * (2 * HEADS * SEQ * 2 * WINDOW * HEAD_DIM)


def tile_hybridattention_pa_kernel(tc, x, Wv, q, k, out):
    nc = tc.nc
    x_rows = x.flatten_outer_dims()
    out_rows = out.flatten_outer_dims()
    q_heads = q.rearrange("b h t d -> (b h) t d")
    k_heads = k.rearrange("b h t d -> (b h) t d")

    with ExitStack() as stack:
        keep = stack.enter_context(tc.tile_pool(name="keep", bufs=1))
        stage = stack.enter_context(tc.tile_pool(name="stage", bufs=4))
        small = stack.enter_context(tc.tile_pool(name="small", bufs=8))
        late = stack.enter_context(tc.tile_pool(name="late", bufs=7))
        pairs = stack.enter_context(tc.tile_pool(name="pairs", bufs=3))
        psum_work = stack.enter_context(tc.psum_pool(name="psum_work", bufs=8))

        w_raw = keep.tile([P, HEADS, FEATURES], BF16)
        k_raw = keep.tile([P, HEADS, ROW_TILES, HEAD_DIM], BF16)
        q_raw = keep.tile([P, HEADS, WINDOWS, TILES_PER_WINDOW, HEAD_DIM], BF16)
        x_raw = keep.tile([P, ROW_TILES // WORD, WORD, FEATURES], BF16)
        def load_keys_and_queries(h, first, last, q_queue=nc.sync):
            nc.sync.dma_start(
                out=k_raw[:, h, TILES_PER_WINDOW * first : TILES_PER_WINDOW * last, :],
                in_=k_heads[h, WINDOW * first : WINDOW * last, :].rearrange("(a p) d -> p a d", p=P),
            )
            q_queue.dma_start(
                out=q_raw[:, h, first:last].rearrange("p w r d -> p w (r d)"),
                in_=q_heads[h, WINDOW * first : WINDOW * last, :].rearrange(
                    "(w p r) d -> p w (r d)", w=last - first, p=P, r=TILES_PER_WINDOW
                ),
            )

        for h in range(HEADS):
            if h == 0:
                load_keys_and_queries(h, 0, 1, q_queue=nc.scalar)
                load_keys_and_queries(h, 1, WINDOWS)
            else:
                load_keys_and_queries(h, 0, WINDOWS)
            nc.sync.dma_start(out=w_raw[:, h, :], in_=Wv[P * h : P * (h + 1), :])
            if h == 0:
                for c in range(ROW_TILES // WORD):
                    nc.sync.dma_start(
                        out=x_raw[:, c],
                        in_=x_rows[WORD * P * c : WORD * P * (c + 1), :].rearrange(
                            "(p e) i -> p e i", e=WORD
                        ),
                    )

        ident_bf16 = keep.tile([P, P], BF16)
        make_identity(nc, ident_bf16[:])
        ident_f32 = keep.tile([P, P], F32)
        make_identity(nc, ident_f32[:])

        zero = keep.tile([P, 1], F32)
        nc.vector.memset(zero[:], 0.0)
        one = keep.tile([P, 1], F32)
        nc.scalar.activation(out=one[:], in_=zero[:], func=EXP)


        w_codes = keep.tile([P, HEADS, FEATURE_PASSES, P], U32, align_bytes=64)
        w_scales = keep.tile([P, HEADS, FEATURE_PASSES, P], U8, align_bytes=64)
        x_codes = keep.tile([P, ROW_TILES, FEATURE_PASSES, P], U32, align_bytes=64)
        x_scales = keep.tile([P, ROW_TILES, FEATURE_PASSES, P], U8, align_bytes=64)

        def rows_entry(rows, codes, scales, by_vector):
            tiles = {}

            def transpose_rows():
                words = rows.bitcast(F32)
                transposed = psum_work.tile([P, WORD_SLABS, P], F32, tag="work")
                for slab in range(WORD_SLABS):
                    nc.tensor.transpose(
                        transposed[:, slab, :], words[:, slab * P : (slab + 1) * P], ident_f32[:]
                    )
                tiles["transposed"] = transposed

            def regroup_rows():
                regrouped = stage.tile([P, FEATURE_PASSES, P, PAIRS], F32, tag="rows", align_bytes=64)
                copy_out = nc.vector.tensor_copy if by_vector else nc.scalar.copy
                copy_out(
                    out=regrouped[:],
                    in_=tiles["transposed"][:].rearrange("p (c u) t -> p c t u", u=PAIRS),
                )
                tiles["regrouped"] = regrouped

            def quantise_rows():
                nc.vector.quantize_mx(
                    out=codes.rearrange("p c t -> p (c t)").bitcast(FP8X4),
                    scales=scales.rearrange("p c t -> p (c t)"),
                    in_=tiles["regrouped"][:].rearrange("p c t u -> p (c t u)").bitcast(BF16),
                )

            copy_stage = "vector copy" if by_vector else "scalar copy"
            return {"matmuls": transpose_rows, copy_stage: regroup_rows, "quantise": quantise_rows}

        v_codes = keep.tile([P, WINDOWS, HEADS, HEAD_DIM], U32, align_bytes=64)
        v_scales = keep.tile([P, WINDOWS, HEADS, HEAD_DIM], U8, align_bytes=64)

        def values_entry(w, h):
            tiles = {}

            def project():
                projected = psum_work.tile([P, PACK, HEAD_DIM], F32, tag="work")
                for j in range(PACK):
                    for c in range(FEATURE_PASSES):
                        nc.tensor.matmul_mx(
                            out=projected[:, j, :],
                            lhsT=x_codes[:, PACK * w + j, c, :].bitcast(FP8X4),
                            lhsT_scale=x_scales[:, PACK * w + j, c, :],
                            rhs=w_codes[:, h, c, :].bitcast(FP8X4),
                            rhs_scale=w_scales[:, h, c, :],
                            start=(c == 0),
                            stop=(c == FEATURE_PASSES - 1),
                        )
                tiles["projected"] = projected

            def regroup_values():
                regrouped = stage.tile([P, HEAD_DIM, PACK], BF16, tag="values", align_bytes=64)
                nc.scalar.copy(
                    out=regrouped[:], in_=tiles["projected"][:].rearrange("p j d -> p d j")
                )
                tiles["regrouped"] = regrouped

            def quantise_values():
                nc.vector.quantize_mx(
                    out=v_codes[:, w, h, :].bitcast(FP8X4),
                    scales=v_scales[:, w, h, :],
                    in_=tiles["regrouped"][:].rearrange("p d j -> p (d j)"),
                )

            return {"matmuls": project, "scalar copy": regroup_values, "quantise": quantise_values}

        kT = keep.tile([P, HEADS, SEQ], BF16)
        qT = keep.tile([P, HEADS, WINDOWS, TILES_PER_WINDOW, P], BF16)

        def head_entry(row_tiles, place):
            tiles = {}

            def transpose_head():
                transposed = psum_work.tile([P, TILES_PER_WINDOW, P], BF16, tag="work")
                for a in range(TILES_PER_WINDOW):
                    nc.tensor.transpose(transposed[:, a, :], row_tiles[:, a, :], ident_bf16[:])
                tiles["transposed"] = transposed

            def keep_head():
                nc.vector.tensor_copy(
                    out=place, in_=tiles["transposed"][:].rearrange("d a p -> d (a p)")
                )

            return {"matmuls": transpose_head, "vector copy": keep_head}

        preparation = []
        values_position = {}

        def add_keys_and_queries(h, w):
            first_tile = TILES_PER_WINDOW * w
            preparation.append(
                head_entry(
                    k_raw[:, h, first_tile : first_tile + TILES_PER_WINDOW, :],
                    kT[:, h, WINDOW * w : WINDOW * (w + 1)],
                )
            )
            preparation.append(
                head_entry(q_raw[:, h, w], qT[:, h, w].rearrange("d r p -> d (r p)"))
            )

        def add_rows_of_wv(h):
            preparation.append(
                rows_entry(
                    w_raw[:, h, :],
                    w_codes[:, h],
                    w_scales[:, h],
                    by_vector=h > 0,
                )
            )

        def add_rows_of_x(w):
            for n in range(TILES_PER_WINDOW * w, TILES_PER_WINDOW * (w + 1)):
                preparation.append(
                    rows_entry(
                        x_raw[:, n // WORD, n % WORD, :],
                        x_codes[:, n],
                        x_scales[:, n],
                        by_vector=n % 4 == 3,
                    )
                )

        def add_values(w, h):
            values_position[(h, w)] = len(preparation)
            preparation.append(values_entry(w, h))

        add_keys_and_queries(0, 0)
        add_keys_and_queries(0, 1)
        add_rows_of_wv(0)
        add_rows_of_x(0)
        add_keys_and_queries(0, 2)
        add_rows_of_x(1)
        for h in range(HEADS):
            add_values(0, h)
            if h < HEADS - 1:
                add_keys_and_queries(h + 1, 0)
            if h == 0:
                add_rows_of_x(2)
            if h < HEADS - 1:
                add_keys_and_queries(h + 1, 1)
            add_values(1, h)
            if h < HEADS - 1:
                add_rows_of_wv(h + 1)
                add_keys_and_queries(h + 1, 2)
            add_values(2, h)
            if h == 0:
                first_head_entries = len(preparation)

        entry_step = []
        for position in range(len(preparation)):
            if position < LEAD:
                entry_step.append(-LEAD)
            elif position < first_head_entries + SPARE:
                entry_step.append((position - LEAD) // 2)
            else:
                entry_step.append(entry_step[-1] + 1)
        started_at = {}
        for position, step in enumerate(entry_step):
            started_at.setdefault(step, []).append(position)

        def prepare(stage_name, start):
            for position in started_at.get(start, []):
                if stage_name in preparation[position]:
                    preparation[position][stage_name]()

        units = []
        for h in range(HEADS):
            for w in range(WINDOWS):
                if w == 0:
                    for r in range(0, TILES_PER_WINDOW, HALVES):
                        units.append((h, w, [(r, 0), (r + 1, 0)]))
                else:
                    for r in range(TILES_PER_WINDOW):
                        units.append((h, w, [(r, 0), (r, w)]))

        score_banks = {}
        row_maxima = {}
        exp_biases = {}
        exponentials = {}
        transposed_e = {}
        regrouped_e = {}
        e_codes = {}
        e_scales = {}
        row_sums = {}
        denominators = {}
        inverses = {}
        products = {}
        results = {}

        def portions(unit):
            if unit == len(units) - 1:
                return [(0, 1), (1, HALVES)]
            return [(0, HALVES)]

        def query_portions(group):
            if group == LAST_GROUP:
                return [(0, TILES_PER_WINDOW - 1), (TILES_PER_WINDOW - 1, TILES_PER_WINDOW)]
            return [(0, TILES_PER_WINDOW)]

        def compute_scores(unit):
            h, w, halves = units[unit]
            score_banks[unit] = []
            for r, kw in halves:
                bank = psum_work.tile([P, WINDOW], F32, tag="work")
                nc.tensor.matmul(
                    out=bank[:],
                    lhsT=qT[:, h, w, r, :],
                    rhs=kT[:, h, WINDOW * kw : WINDOW * (kw + 1)],
                    start=True,
                    stop=True,
                )
                score_banks[unit].append(bank)

        def find_maxima(unit):
            maxima = small.tile([P, HALVES], F32, tag="maxima")
            for g, bank in enumerate(score_banks[unit]):
                nc.vector.tensor_reduce(
                    out=maxima[:, g : g + 1], in_=bank[:], axis=AXIS_X, op=ALU.max
                )
            row_maxima[unit] = maxima

        def make_bias(unit):
            w = units[unit][1]
            maxima = row_maxima[unit]
            bias = small.tile([P, HALVES], F32, tag="bias")
            if w == 0:
                for g in range(HALVES):
                    nc.gpsimd.tensor_scalar(
                        out=bias[:, g : g + 1],
                        in0=maxima[:, g : g + 1],
                        scalar1=-SCALE,
                        scalar2=0.0,
                        op0=ALU.mult,
                        op1=ALU.add,
                    )
            else:
                nc.gpsimd.tensor_scalar(
                    out=bias[:, 0:1],
                    in0=maxima[:, 0:1],
                    scalar1=maxima[:, 1:2],
                    scalar2=-SCALE,
                    op0=ALU.max,
                    op1=ALU.mult,
                )
            exp_biases[unit] = bias

        def exponentiate(unit):
            h, w, halves = units[unit]
            if halves[0][0] == 0:
                sums = small.tile([P, TILES_PER_WINDOW, HALVES], F32, tag="sums")
                row_sums[(h, w)] = sums
            e = stage.tile([P, HALVES * WINDOW], BF16, tag="e")
            for g, bank in enumerate(score_banks[unit]):
                r = halves[g][0]
                bias_column = g if w == 0 else 0
                part = 0 if w == 0 else g
                nc.scalar.activation(
                    out=e[:, WINDOW * g : WINDOW * (g + 1)],
                    in_=bank[:],
                    func=EXP,
                    bias=exp_biases[unit][:, bias_column : bias_column + 1],
                    scale=SCALE,
                    accum_out=row_sums[(h, w)][:, r, part : part + 1],
                )
            exponentials[unit] = e

        def transpose_e(unit, first, last):
            words = exponentials[unit][:].bitcast(F32)
            transposed = psum_work.tile([P, HALVES, PAIRS, P], F32, tag="work")
            for g in range(first, last):
                for u in range(PAIRS):
                    slab = PAIRS * g + u
                    nc.tensor.transpose(
                        transposed[:, g, u, :], words[:, slab * P : (slab + 1) * P], ident_f32[:]
                    )
            transposed_e[(unit, first)] = transposed

        def regroup_e(unit, first, last):
            if unit % 2 == 0:
                pair = pairs.tile([P, 2, HALVES, P, PAIRS], F32, tag="regrouped_e", align_bytes=64)
                regrouped_e[unit // 2] = pair
            regrouped = regrouped_e[unit // 2][:, unit % 2]
            by_vector = len(units) - 3 <= unit < len(units) - 1 or unit == len(units) - UNITS_PER_HEAD + 1
            copy_out = nc.vector.tensor_copy if by_vector else nc.scalar.copy
            copy_out(
                out=regrouped[:, first:last],
                in_=transposed_e[(unit, first)][:, first:last].rearrange("p g u q -> p g q u"),
            )

        def quantise_e(unit, first, last):
            last_pair = unit >= len(units) - 2
            if unit % 2 == 0:
                codes = late.tile([P, 2, HALVES, P], U32, tag="e_codes", align_bytes=64)
                scales = late.tile([P, 2, HALVES, P], U8, tag="e_scales", align_bytes=64)
                for n in range(2):
                    e_codes[unit + n] = codes[:, n]
                    e_scales[unit + n] = scales[:, n]
                e_codes[(unit // 2, "pair")] = codes
                e_scales[(unit // 2, "pair")] = scales
            if last_pair:
                nc.vector.quantize_mx(
                    out=e_codes[unit][:, first:last].rearrange("p g q -> p (g q)").bitcast(FP8X4),
                    scales=e_scales[unit][:, first:last].rearrange("p g q -> p (g q)"),
                    in_=regrouped_e[unit // 2][:, unit % 2, first:last]
                    .rearrange("p g q u -> p (g q u)")
                    .bitcast(BF16),
                )
            elif unit % 2 == 1:
                nc.vector.quantize_mx(
                    out=e_codes[(unit // 2, "pair")][:].rearrange("p n g q -> p (n g q)").bitcast(FP8X4),
                    scales=e_scales[(unit // 2, "pair")][:].rearrange("p n g q -> p (n g q)"),
                    in_=regrouped_e[unit // 2][:].rearrange("p n g q u -> p (n g q u)").bitcast(BF16),
                )

        def multiply_by_v(unit, first, last):
            h, w, halves = units[unit]
            for first_tile, last_tile in query_portions((h, w)):
                if halves[0][0] == first_tile and first == 0:
                    product = psum_work.tile([P, TILES_PER_WINDOW, HEAD_DIM], F32, tag="work")
                    for r in range(first_tile, last_tile):
                        products[(h, w, r)] = product
            for g in range(first, last):
                r, kw = halves[g]
                nc.tensor.matmul_mx(
                    out=products[(h, w, r)][:, r, :],
                    lhsT=e_codes[unit][:, g, :].bitcast(FP8X4),
                    lhsT_scale=e_scales[unit][:, g, :],
                    rhs=v_codes[:, kw, h, :].bitcast(FP8X4),
                    rhs_scale=v_scales[:, kw, h, :],
                    start=(w == 0 or g == 0),
                    stop=(w == 0 or g == HALVES - 1),
                )

        def add_row_sums(group, first, last):
            sums = row_sums[group]
            if group[1] == 0:
                denominators[group] = sums[:, :, 0]
            else:
                if first == 0:
                    total = small.tile([P, TILES_PER_WINDOW], F32, tag="total")
                    denominators[group] = total[:]
                nc.gpsimd.tensor_tensor(
                    out=denominators[group][:, first:last],
                    in0=sums[:, first:last, 0],
                    in1=sums[:, first:last, 1],
                    op=ALU.add,
                )

        def invert_row_sums(group, first, last):
            if first == 0:
                inverse = small.tile([P, TILES_PER_WINDOW], F32, tag="inverse")
                inverses[group] = inverse
            nc.vector.reciprocal(
                out=inverses[group][:, first:last], in_=denominators[group][:, first:last]
            )

        def divide_and_store(group, first, last):
            h, w = group
            if first == 0:
                result = stage.tile([P, TILES_PER_WINDOW, HEAD_DIM], F32, tag="result")
                results[group] = result
            nc.vector.tensor_tensor(
                out=results[group][:, first:last],
                in0=products[(h, w, first)][:, first:last],
                in1=inverses[group][:, first:last].unsqueeze(2).to_broadcast([P, last - first, HEAD_DIM]),
                op=ALU.mult,
            )
            nc.sync.dma_start(
                out=out_rows[
                    WINDOW * w : WINDOW * (w + 1), HEAD_DIM * h : HEAD_DIM * (h + 1)
                ].rearrange("(p r) d -> p r d", r=TILES_PER_WINDOW)[:, first:last],
                in_=results[group][:, first:last],
            )

        products_at = {}
        divide_at = {}
        step = 0
        group_units = []
        for unit, (h, w, halves) in enumerate(units):
            group_units.append((unit, 0, HALVES))
            ready = max(entry_step[values_position[(h, kw)]] for r, kw in halves) + 2
            if (h, w) == LAST_GROUP:
                for number, (first, last) in enumerate(portions(unit)):
                    step = unit + PRODUCT_LAG + number
                    products_at[step] = [(unit, first, last)]
            elif halves[1][0] == TILES_PER_WINDOW - 1:
                step = max(step + 1, unit + PRODUCT_LAG, ready)
                products_at[step] = group_units
                group_units = []
            for first, last in query_portions((h, w)):
                if halves[1][0] == last - 1:
                    divide_at.setdefault(step + 1, []).append(((h, w), first, last))

        def for_unit(stage_fn, unit):
            if 0 <= unit < len(units):
                stage_fn(unit)

        def for_portions(stage_fn, unit):
            for number in range(HALVES):
                if 0 <= unit - number < len(units) and number < len(portions(unit - number)):
                    stage_fn(unit - number, *portions(unit - number)[number])

        def for_query_portions(stage_fn, unit):
            if 0 <= unit < len(units):
                h, w, halves = units[unit]
                for first, last in query_portions((h, w)):
                    if halves[1][0] == last - 1:
                        stage_fn((h, w), first, last)

        stack.enter_context(tc.manual_schedule())
        for step in range(FIRST_STEP, max(divide_at) + 1):
            for_unit(find_maxima, step - MAXIMA_LAG)
            for_unit(make_bias, step - MAXIMA_LAG)
            prepare("vector copy", step - 1)
            for_unit(exponentiate, step - EXP_LAG)
            prepare("scalar copy", step - 1)
            for_query_portions(add_row_sums, step - REGROUP_LAG)
            prepare("quantise", step - 2)
            for_query_portions(invert_row_sums, step - QUANTISE_LAG)
            for_portions(quantise_e, step - QUANTISE_LAG)
            for group, first, last in divide_at.get(step, []):
                divide_and_store(group, first, last)
            for_portions(regroup_e, step - REGROUP_LAG)
            for_unit(compute_scores, step)
            prepare("matmuls", step)
            for unit, first, last in products_at.get(step, []):
                multiply_by_v(unit, first, last)
            for_portions(transpose_e, step - EXP_LAG)
